import numpy as np
import ml_dtypes


def mxq(x, axis, fmt="e4m3"):
    dtype, down = {"e4m3": (ml_dtypes.float8_e4m3fn, 7), "e5m2": (ml_dtypes.float8_e5m2, 14)}[fmt]
    v = np.moveaxis(np.asarray(x, np.float32).astype(ml_dtypes.bfloat16).astype(np.float64), axis, -1)
    blocks = v.reshape(v.shape[:-1] + (-1, 32))
    amax = np.abs(blocks).max(-1, keepdims=True)
    byte = np.maximum(np.where(amax > 0, np.frexp(amax)[1] - 1 + 127, 0) - down, 1)
    scale = np.exp2(byte - 127.0)
    codes = (blocks / scale).astype(np.float32).astype(dtype).astype(np.float64)
    return np.moveaxis((codes * scale).reshape(v.shape), -1, axis)


WIDE = False


def mx_kscale(k):
    if not WIDE:
        return np.ones(k)
    levels = np.array([10, -10, 5, -5, 0])
    a = np.random.permutation(np.resize(levels, k // 512 * 4)).reshape(k // 512, 4)
    idx = np.arange(k)
    return np.exp2(a[idx // 512, idx % 128 // 32])


BF16 = ml_dtypes.bfloat16


def bf(x):
    return np.asarray(x, np.float32).astype(BF16)


def f64(x):
    return np.asarray(x).astype(np.float64)


B, IN, OUT, M = 8192, 1024, 256, 512
SW = 0.05 * M / np.sqrt(IN)


def setup_inputs():
    r = mx_kscale(M)
    r = r / r.min()
    rn = r / r.max()
    x = np.random.standard_normal((B, IN)) * 0.5 * r.max()
    mus = np.random.uniform(size=(M, 2))
    log_vars = np.log((1.0 / np.sqrt(M)) ** 2) - np.random.uniform(size=(M, 2))
    log_vars[:, 1] += 2.0 * np.log(r)
    u = np.random.uniform(size=M) - 0.5
    u = u - (np.sum(u * rn) - SW) / np.sum(rn)
    return {"x": bf(x), "mus": bf(mus), "log_vars": bf(log_vars), "weights": bf(u * rn)}


def reference(x, mus, log_vars, weights):
    x, mus, log_vars, weights = f64(x), f64(mus), f64(log_vars), f64(weights)
    vars_ = np.exp(log_vars)
    x_in_idx = np.linspace(0.0, 1.0, IN)
    x_out_idx = np.linspace(0.0, 1.0, OUT)
    inv_norm = 1.0 / np.sqrt(2.0 * np.pi * vars_)
    g_in = np.exp(-(x_in_idx[:, None] - mus[None, :, 0]) ** 2 / (2.0 * vars_[None, :, 0])) * inv_norm[None, :, 0]
    C = (mxq(x, 1, "e4m3") @ mxq(g_in, 0, "e4m3")) * weights
    g_out = np.exp(-(x_out_idx[None, :] - mus[:, 1:2]) ** 2 / (2.0 * vars_[:, 1:2])) * inv_norm[:, 1:2]
    return (mxq(C, 1, "e4m3") @ mxq(g_out, 0, "e4m3")) / (IN * np.sum(weights))

@@ -1,0 +1,316 @@
+import math
+from contextlib import ExitStack
+
+import concourse.mybir as mybir
+from concourse.masks import make_identity
+
+F32 = mybir.dt.float32
+BF16 = mybir.dt.bfloat16
+I32 = mybir.dt.int32
+U32 = mybir.dt.uint32
+U8 = mybir.dt.uint8
+FP8X4 = mybir.dt.float8_e4m3fn_x4
+ACT = mybir.ActivationFunctionType
+ALU = mybir.AluOpType
+
+BATCH, IN, OUT, COMPS = 8192, 1024, 256, 512
+FLOPS = 2 * BATCH * IN * COMPS + 2 * BATCH * COMPS * OUT
+
+P = 128
+PACK = 4
+K_PASS = P * PACK
+PASSES = IN // K_PASS
+ROWS = 4
+CHUNK = ROWS * P
+N_CHUNKS = BATCH // CHUNK
+X_BUFS = 12
+LOOKAHEAD = 2
+
+ROUND_AND_BIAS = 1.5 * 2.0**23 + 127.0
+LN2_HI = 0.693145751953125
+LN2_LO = math.log(2.0) - LN2_HI
+EXP_DEGREE = 8
+
+
+def factorial(n):
+    product = 1
+    for factor in range(2, n + 1):
+        product *= factor
+    return product
+
+
+def tile_gaussianlayer_t_kernel(tc, x, mus, log_vars, weights, out):
+    nc = tc.nc
+    with ExitStack() as ctx:
+        keep = ctx.enter_context(tc.tile_pool(name="keep", bufs=1))
+        x_pool = ctx.enter_context(tc.tile_pool(name="x_pool", bufs=X_BUFS))
+        stream = ctx.enter_context(tc.tile_pool(name="stream", bufs=3))
+        psum_x = ctx.enter_context(tc.psum_pool(name="psum_x", bufs=3))
+        psum_c = ctx.enter_context(tc.psum_pool(name="psum_c", bufs=3))
+        psum_o = ctx.enter_context(tc.psum_pool(name="psum_o", bufs=2))
+
+        mus_sb = keep.tile([P, PACK * 2], BF16, name="mus_sb")
+        nc.sync.dma_start(out=mus_sb[:], in_=mus.rearrange("(p t) c -> p (t c)", t=PACK))
+        lv_sb = keep.tile([P, PACK * 2], BF16, name="lv_sb")
+        nc.sync.dma_start(out=lv_sb[:], in_=log_vars.rearrange("(p t) c -> p (t c)", t=PACK))
+        w_sb = keep.tile([P, PACK], BF16, name="w_sb")
+        nc.sync.dma_start(out=w_sb[:], in_=weights.rearrange("(p t) -> p t", t=PACK))
+
+        x_tiles = {}
+
+        def load_chunk(c):
+            x_sb = x_pool.tile([P, ROWS * IN], BF16, name="x_sb")
+            rows = x[c * CHUNK : (c + 1) * CHUNK, :]
+            nc.sync.dma_start(out=x_sb[:], in_=rows.rearrange("(p r) k -> p (r k)", r=ROWS))
+            x_tiles[c] = x_sb
+
+        for c in range(X_BUFS):
+            load_chunk(c)
+
+        ident_f32 = keep.tile([P, P], F32, name="ident_f32")
+        make_identity(nc, ident_f32[:])
+        k_row = keep.tile([P, IN], F32, name="k_row")
+        nc.gpsimd.iota(
+            k_row[:],
+            pattern=[[2 * P, IN // (2 * P)], [1, 2], [2, P]],
+            base=0,
+            channel_multiplier=0,
+            allow_small_or_imprecise_dtypes=True,
+        )
+        ident_bf = keep.tile([P, P], BF16, name="ident_bf")
+        make_identity(nc, ident_bf[:])
+        ones_bf = keep.tile([P, P], BF16, name="ones_bf")
+        nc.vector.memset(ones_bf[:], 1.0)
+        warm = keep.tile([P, 1], F32, name="warm")
+        nc.vector.memset(warm[:], 0.0)
+        warm_out = keep.tile([P, 1], F32, name="warm_out")
+        nc.scalar.activation(out=warm_out[:], in_=warm[:], func=ACT.Exp)
+
+        def by_axis(tile_ap, axis):
+            return tile_ap.rearrange("p (t a) -> p t a", a=2)[:, :, axis]
+
+        spans = (IN - 1, OUT - 1)
+        neg_centre = keep.tile([P, PACK * 2], F32, name="neg_centre")
+        for axis, span in enumerate(spans):
+            nc.vector.tensor_scalar(
+                out=by_axis(neg_centre[:], axis), in0=by_axis(mus_sb[:], axis),
+                scalar1=-float(span), scalar2=None, op0=ALU.mult,
+            )
+
+        sq_in = []
+        for t in range(PACK):
+            sq = keep.tile([P, IN], F32, name="sq%d" % t)
+            nc.scalar.activation(
+                out=sq[:], in_=k_row[:], func=ACT.Square, bias=neg_centre[:, 2 * t : 2 * t + 1], scale=1.0
+            )
+            sq_in.append(sq)
+
+        shifted = keep.tile([P, PACK * 2], F32, name="shifted")
+        nc.vector.tensor_scalar(
+            out=shifted[:], in0=lv_sb[:], scalar1=-1.0 / math.log(2.0), scalar2=ROUND_AND_BIAS,
+            op0=ALU.mult, op1=ALU.add,
+        )
+        n_f32 = keep.tile([P, PACK * 2], F32, name="n_f32")
+        nc.vector.tensor_scalar(out=n_f32[:], in0=shifted[:], scalar1=ROUND_AND_BIAS, scalar2=None, op0=ALU.subtract)
+        rem = keep.tile([P, PACK * 2], F32, name="rem")
+        nc.vector.scalar_tensor_tensor(
+            out=rem[:], in0=n_f32[:], scalar=-LN2_HI, in1=lv_sb[:], op0=ALU.mult, op1=ALU.subtract
+        )
+        nc.vector.scalar_tensor_tensor(
+            out=rem[:], in0=n_f32[:], scalar=-LN2_LO, in1=rem[:], op0=ALU.mult, op1=ALU.add
+        )
+        series = keep.tile([P, PACK * 2], F32, name="series")
+        nc.vector.tensor_scalar(
+            out=series[:], in0=rem[:], scalar1=1.0 / factorial(EXP_DEGREE), scalar2=None, op0=ALU.mult
+        )
+        for degree in range(EXP_DEGREE - 1, 0, -1):
+            nc.vector.scalar_tensor_tensor(
+                out=series[:], in0=series[:], scalar=1.0 / factorial(degree), in1=rem[:],
+                op0=ALU.add, op1=ALU.mult,
+            )
+        two_to_n = keep.tile([P, PACK * 2], I32, name="two_to_n")
+        nc.vector.tensor_single_scalar(
+            out=two_to_n[:], in_=shifted[:].bitcast(I32), scalar=23, op=ALU.logical_shift_left
+        )
+        scaled = keep.tile([P, PACK * 2], F32, name="scaled")
+        for axis, span in enumerate(spans):
+            nc.vector.tensor_scalar(
+                out=by_axis(scaled[:], axis), in0=by_axis(two_to_n[:].bitcast(F32), axis),
+                scalar1=-0.5 / float(span * span), scalar2=None, op0=ALU.mult,
+            )
+        neg_steep = keep.tile([P, PACK * 2], F32, name="neg_steep")
+        nc.vector.scalar_tensor_tensor(
+            out=neg_steep[:], in0=series[:], scalar=1.0, in1=scaled[:], op0=ALU.add, op1=ALU.mult
+        )
+        log_norm = keep.tile([P, PACK * 2], F32, name="log_norm")
+        nc.vector.tensor_scalar(
+            out=log_norm[:], in0=lv_sb[:], scalar1=-0.5, scalar2=-0.5 * math.log(2.0 * math.pi),
+            op0=ALU.mult, op1=ALU.add,
+        )
+        w_f32 = keep.tile([P, PACK], F32, name="w_f32")
+        nc.vector.tensor_copy(out=w_f32[:], in_=w_sb[:])
+
+        w_ps = psum_o.tile([P, 2 * OUT], F32, name="w_ps", tag="o_ps")
+        nc.tensor.matmul(out=w_ps[:, 0:PACK], lhsT=ones_bf[:], rhs=w_sb[:], start=True, stop=True)
+        w_sum = keep.tile([P, 1], F32, name="w_sum")
+        nc.vector.reduce_sum(out=w_sum[:], in_=w_ps[:, 0:PACK], axis=mybir.AxisListType.X)
+        divisor = keep.tile([P, 1], F32, name="divisor")
+        nc.vector.tensor_scalar(out=divisor[:], in0=w_sum[:], scalar1=float(IN), scalar2=None, op0=ALU.mult)
+        inv_divisor = keep.tile([P, 1], F32, name="inv_divisor")
+        nc.vector.reciprocal(out=inv_divisor[:], in_=divisor[:])
+
+        gx_tiles, xc_tiles, xs_tiles = {}, {}, {}
+        gc_tiles, cc_tiles, cs_tiles = {}, {}, {}
+        o_banks = {}
+
+        def transpose_chunk(c):
+            words = x_tiles[c][:].bitcast(F32)
+            gx = stream.tile([P, ROWS * IN], BF16, name="gx", align_bytes=64)
+            gx_words = gx[:].bitcast(F32)
+            half = IN // 2
+            for r in range(ROWS):
+                xt = psum_x.tile([P, PACK, P], F32, name="xt", tag="xt")
+                for q in range(PACK):
+                    first = r * half + q * P
+                    nc.tensor.transpose(xt[:, q, :], words[:, first : first + P], ident_f32[:])
+                nc.scalar.copy(
+                    out=gx_words[:, r * half : (r + 1) * half].rearrange("p (g b u) -> p g b u", g=PASSES, u=2),
+                    in_=xt[:].rearrange("p (g u) b -> p g b u", u=2),
+                )
+            gx_tiles[c] = gx
+
+        def quantise_x(c):
+            xc = stream.tile([P, ROWS * PASSES * P], U32, name="xc", align_bytes=64, bufs=LOOKAHEAD + 2)
+            xs = stream.tile([P, ROWS * PASSES * P], U8, name="xs", align_bytes=64, bufs=LOOKAHEAD + 2)
+            nc.vector.quantize_mx(out=xc[:].bitcast(FP8X4), scales=xs[:], in_=gx_tiles[c][:])
+            xc_tiles[c], xs_tiles[c] = xc, xs
+
+        def first_matmul(c, r):
+            if r == 0:
+                gc_tiles[c] = stream.tile([P, ROWS * COMPS], BF16, name="gc", align_bytes=64)
+            c_ps = psum_c.tile([P, PACK, P], F32, name="c_ps")
+            for t in range(PACK):
+                for g in range(PASSES):
+                    w_cols = slice((t * PASSES + g) * P, (t * PASSES + g + 1) * P)
+                    x_cols = slice((r * PASSES + g) * P, (r * PASSES + g + 1) * P)
+                    nc.tensor.matmul_mx(
+                        out=c_ps[:, t, :],
+                        lhsT=gin_c[:, w_cols].bitcast(FP8X4),
+                        lhsT_scale=gin_s[:, w_cols],
+                        rhs=xc_tiles[c][:, x_cols].bitcast(FP8X4),
+                        rhs_scale=xs_tiles[c][:, x_cols],
+                        start=(g == 0),
+                        stop=(g == PASSES - 1),
+                    )
+            nc.vector.tensor_tensor(
+                out=gc_tiles[c][:, r * COMPS : (r + 1) * COMPS].rearrange("p (b t) -> p b t", t=PACK),
+                in0=c_ps[:].rearrange("p t b -> p b t"),
+                in1=w_f32[:].unsqueeze(1).to_broadcast([P, P, PACK]),
+                op=ALU.mult,
+            )
+
+        def quantise_c(c):
+            cc = stream.tile([P, ROWS * P], U32, name="cc", align_bytes=64)
+            cs = stream.tile([P, ROWS * P], U8, name="cs", align_bytes=64)
+            nc.vector.quantize_mx(out=cc[:].bitcast(FP8X4), scales=cs[:], in_=gc_tiles[c][:])
+            cc_tiles[c], cs_tiles[c] = cc, cs
+
+        def second_matmul(c):
+            o_banks[c] = []
+            for h in range(ROWS // 2):
+                o_ps = psum_o.tile([P, 2 * OUT], F32, name="o_ps", tag="o_ps")
+                for s in range(2):
+                    b_cols = slice((2 * h + s) * P, (2 * h + s + 1) * P)
+                    nc.tensor.matmul_mx(
+                        out=o_ps[:, s * OUT : (s + 1) * OUT],
+                        lhsT=cc_tiles[c][:, b_cols].bitcast(FP8X4),
+                        lhsT_scale=cs_tiles[c][:, b_cols],
+                        rhs=gout_c[:].bitcast(FP8X4),
+                        rhs_scale=gout_s[:],
+                        start=True,
+                        stop=True,
+                    )
+                o_banks[c].append(o_ps)
+
+        def store_chunk(c):
+            o_sb = stream.tile([P, ROWS * OUT], F32, name="o_sb")
+            for h, o_ps in enumerate(o_banks[c]):
+                nc.scalar.activation(
+                    out=o_sb[:, 2 * h * OUT : 2 * (h + 1) * OUT], in_=o_ps[:], func=ACT.Copy,
+                    scale=inv_divisor[:, 0:1],
+                )
+            rows = out[c * CHUNK : (c + 1) * CHUNK, :]
+            nc.sync.dma_start(out=rows.rearrange("(p r) j -> p (r j)", r=ROWS), in_=o_sb[:])
+
+        transpose_chunk(0)
+        quantise_x(0)
+
+        gg_in = keep.tile([P, PACK * PASSES * P * PACK], BF16, name="gg_in", align_bytes=64)
+        gin_c = keep.tile([P, PACK * PASSES * P], U32, name="gin_c", align_bytes=64)
+        gin_s = keep.tile([P, PACK * PASSES * P], U8, name="gin_s", align_bytes=64)
+        for t in range(PACK):
+            col = 2 * t
+            g_t = stream.tile([P, IN], BF16, name="g_t", bufs=2)
+            nc.scalar.activation(
+                out=g_t[:], in_=sq_in[t][:], func=ACT.Exp, bias=log_norm[:, col : col + 1],
+                scale=neg_steep[:, col : col + 1],
+            )
+            g_ps = psum_x.tile([P, PASSES * PACK, P], BF16, name="g_ps", tag="xt")
+            for j in range(PASSES * PACK):
+                nc.tensor.transpose(g_ps[:, j, :], g_t[:, j * P : (j + 1) * P], ident_bf[:])
+            nc.vector.tensor_copy(
+                out=gg_in[:, t * IN : (t + 1) * IN].rearrange("p (g m k) -> p g m k", g=PASSES, k=PACK),
+                in_=g_ps[:].rearrange("p (g k) m -> p g m k", k=PACK),
+            )
+            words = slice(t * PASSES * P, (t + 1) * PASSES * P)
+            nc.vector.quantize_mx(
+                out=gin_c[:, words].bitcast(FP8X4), scales=gin_s[:, words], in_=gg_in[:, t * IN : (t + 1) * IN]
+            )
+
+        for c in range(1, LOOKAHEAD):
+            transpose_chunk(c)
+            quantise_x(c)
+
+        planes = keep.tile([P, PACK, OUT], BF16, name="planes")
+        for t in range(PACK):
+            col = 2 * t + 1
+            sq_o = stream.tile([P, OUT], F32, name="sq_o", bufs=2)
+            nc.scalar.activation(
+                out=sq_o[:].rearrange("p (s e) -> p s e", e=2),
+                in_=k_row[:, 0:OUT].rearrange("p (e s) -> p s e", e=2),
+                func=ACT.Square, bias=neg_centre[:, col : col + 1], scale=1.0,
+            )
+            nc.scalar.activation(
+                out=planes[:, t, :], in_=sq_o[:], func=ACT.Exp, bias=log_norm[:, col : col + 1],
+                scale=neg_steep[:, col : col + 1],
+            )
+        gg_out = keep.tile([P, OUT, PACK], BF16, name="gg_out", align_bytes=64)
+        gout_c = keep.tile([P, OUT], U32, name="gout_c", align_bytes=64)
+        gout_s = keep.tile([P, OUT], U8, name="gout_s", align_bytes=64)
+
+        def quantise_g_out():
+            nc.vector.tensor_copy(out=gg_out[:], in_=planes[:].rearrange("p t j -> p j t"))
+            nc.vector.quantize_mx(
+                out=gout_c[:].bitcast(FP8X4), scales=gout_s[:], in_=gg_out[:].rearrange("p j t -> p (j t)")
+            )
+
+        for i in range(N_CHUNKS + 2):
+            if i + X_BUFS < N_CHUNKS:
+                load_chunk(i + X_BUFS)
+            if i + LOOKAHEAD < N_CHUNKS:
+                transpose_chunk(i + LOOKAHEAD)
+            if i >= 2:
+                store_chunk(i - 2)
+            if i < N_CHUNKS:
+                for r in range(ROWS):
+                    first_matmul(i, r)
+                    if r == 0 and i >= 1:
+                        quantise_c(i - 1)
+                    if r == 2 and i + LOOKAHEAD < N_CHUNKS:
+                        quantise_x(i + LOOKAHEAD)
+                if i == 0:
+                    quantise_g_out()
+            if i == N_CHUNKS:
+                quantise_c(i - 1)
+            if 1 <= i <= N_CHUNKS:
+                second_matmul(i - 1)

@@ -48,6 +48,7 @@ def tile_gaussianlayer_t_kernel(tc, x, mus, log_vars, weights, out):
         psum_x = ctx.enter_context(tc.psum_pool(name="psum_x", bufs=3))
         psum_c = ctx.enter_context(tc.psum_pool(name="psum_c", bufs=3))
         psum_o = ctx.enter_context(tc.psum_pool(name="psum_o", bufs=2))
+        ctx.enter_context(tc.manual_schedule())
 
         mus_sb = keep.tile([P, PACK * 2], BF16, name="mus_sb")
         nc.sync.dma_start(out=mus_sb[:], in_=mus.rearrange("(p t) c -> p (t c)", t=PACK))
@@ -272,23 +273,23 @@ def tile_gaussianlayer_t_kernel(tc, x, mus, log_vars, weights, out):
             quantise_x(c)
 
         planes = keep.tile([P, PACK, OUT], BF16, name="planes")
-        for t in range(PACK):
-            col = 2 * t + 1
-            sq_o = stream.tile([P, OUT], F32, name="sq_o", bufs=2)
-            nc.scalar.activation(
-                out=sq_o[:].rearrange("p (s e) -> p s e", e=2),
-                in_=k_row[:, 0:OUT].rearrange("p (e s) -> p s e", e=2),
-                func=ACT.Square, bias=neg_centre[:, col : col + 1], scale=1.0,
-            )
-            nc.scalar.activation(
-                out=planes[:, t, :], in_=sq_o[:], func=ACT.Exp, bias=log_norm[:, col : col + 1],
-                scale=neg_steep[:, col : col + 1],
-            )
         gg_out = keep.tile([P, OUT, PACK], BF16, name="gg_out", align_bytes=64)
         gout_c = keep.tile([P, OUT], U32, name="gout_c", align_bytes=64)
         gout_s = keep.tile([P, OUT], U8, name="gout_s", align_bytes=64)
 
-        def quantise_g_out():
+        def make_g_out():
+            for t in range(PACK):
+                col = 2 * t + 1
+                sq_o = stream.tile([P, OUT], F32, name="sq_o", bufs=2)
+                nc.scalar.activation(
+                    out=sq_o[:].rearrange("p (s e) -> p s e", e=2),
+                    in_=k_row[:, 0:OUT].rearrange("p (e s) -> p s e", e=2),
+                    func=ACT.Square, bias=neg_centre[:, col : col + 1], scale=1.0,
+                )
+                nc.scalar.activation(
+                    out=planes[:, t, :], in_=sq_o[:], func=ACT.Exp, bias=log_norm[:, col : col + 1],
+                    scale=neg_steep[:, col : col + 1],
+                )
             nc.vector.tensor_copy(out=gg_out[:], in_=planes[:].rearrange("p t j -> p j t"))
             nc.vector.quantize_mx(
                 out=gout_c[:].bitcast(FP8X4), scales=gout_s[:], in_=gg_out[:].rearrange("p j t -> p (j t)")
@@ -309,7 +310,7 @@ def tile_gaussianlayer_t_kernel(tc, x, mus, log_vars, weights, out):
                     if r == 2 and i + LOOKAHEAD < N_CHUNKS:
                         quantise_x(i + LOOKAHEAD)
                 if i == 0:
-                    quantise_g_out()
+                    make_g_out()
             if i == N_CHUNKS:
                 quantise_c(i - 1)
             if 1 <= i <= N_CHUNKS:

@@ -21,6 +21,8 @@ PACK = 4
 K_PASS = P * PACK
 PASSES = IN // K_PASS
 ROWS = 4
+HALVES = 2
+HALF_ROWS = ROWS // HALVES
 CHUNK = ROWS * P
 N_CHUNKS = BATCH // CHUNK
 X_BUFS = 12
@@ -68,24 +70,26 @@ def tile_gaussianlayer_t_kernel(tc, x, mus, log_vars, weights, out):
         for c in range(X_BUFS):
             load_chunk(c)
 
-        ident_f32 = keep.tile([P, P], F32, name="ident_f32")
-        make_identity(nc, ident_f32[:])
-        k_row = keep.tile([P, IN], F32, name="k_row")
-        nc.gpsimd.iota(
-            k_row[:],
-            pattern=[[2 * P, IN // (2 * P)], [1, 2], [2, P]],
-            base=0,
-            channel_multiplier=0,
-            allow_small_or_imprecise_dtypes=True,
-        )
-        ident_bf = keep.tile([P, P], BF16, name="ident_bf")
-        make_identity(nc, ident_bf[:])
         ones_bf = keep.tile([P, P], BF16, name="ones_bf")
         nc.vector.memset(ones_bf[:], 1.0)
         warm = keep.tile([P, 1], F32, name="warm")
         nc.vector.memset(warm[:], 0.0)
         warm_out = keep.tile([P, 1], F32, name="warm_out")
         nc.scalar.activation(out=warm_out[:], in_=warm[:], func=ACT.Exp)
+        k_row = keep.tile([P, IN], F32, name="k_row")
+        nc.gpsimd.iota(
+            k_row[:, 0 : 2 * P], pattern=[[1, 2], [2, P]], base=0, channel_multiplier=0,
+            allow_small_or_imprecise_dtypes=True,
+        )
+        for q in range(1, IN // (2 * P)):
+            nc.vector.tensor_scalar(
+                out=k_row[:, q * 2 * P : (q + 1) * 2 * P], in0=k_row[:, 0 : 2 * P],
+                scalar1=float(q * 2 * P), scalar2=None, op0=ALU.add,
+            )
+        ident_f32 = keep.tile([P, P], F32, name="ident_f32")
+        make_identity(nc, ident_f32[:])
+        ident_bf = keep.tile([P, P], BF16, name="ident_bf")
+        make_identity(nc, ident_bf[:])
 
         def by_axis(tile_ap, axis):
             return tile_ap.rearrange("p (t a) -> p t a", a=2)[:, :, axis]
@@ -151,7 +155,7 @@ def tile_gaussianlayer_t_kernel(tc, x, mus, log_vars, weights, out):
         w_f32 = keep.tile([P, PACK], F32, name="w_f32")
         nc.vector.tensor_copy(out=w_f32[:], in_=w_sb[:])
 
-        w_ps = psum_o.tile([P, 2 * OUT], F32, name="w_ps", tag="o_ps")
+        w_ps = psum_o.tile([P, HALF_ROWS * OUT], F32, name="w_ps", tag="o_ps")
         nc.tensor.matmul(out=w_ps[:, 0:PACK], lhsT=ones_bf[:], rhs=w_sb[:], start=True, stop=True)
         w_sum = keep.tile([P, 1], F32, name="w_sum")
         nc.vector.reduce_sum(out=w_sum[:], in_=w_ps[:, 0:PACK], axis=mybir.AxisListType.X)
@@ -164,17 +168,17 @@ def tile_gaussianlayer_t_kernel(tc, x, mus, log_vars, weights, out):
         gc_tiles, cc_tiles, cs_tiles = {}, {}, {}
         o_banks = {}
 
-        def transpose_chunk(c):
+        def transpose_chunk(c, copy_out):
             words = x_tiles[c][:].bitcast(F32)
             gx = stream.tile([P, ROWS * IN], BF16, name="gx", align_bytes=64)
             gx_words = gx[:].bitcast(F32)
             half = IN // 2
             for r in range(ROWS):
-                xt = psum_x.tile([P, PACK, P], F32, name="xt", tag="xt")
+                xt = psum_x.tile([P, PACK, P], F32, name="xt")
                 for q in range(PACK):
                     first = r * half + q * P
                     nc.tensor.transpose(xt[:, q, :], words[:, first : first + P], ident_f32[:])
-                nc.scalar.copy(
+                copy_out(
                     out=gx_words[:, r * half : (r + 1) * half].rearrange("p (g b u) -> p g b u", g=PASSES, u=2),
                     in_=xt[:].rearrange("p (g u) b -> p g b u", u=2),
                 )
@@ -189,7 +193,9 @@ def tile_gaussianlayer_t_kernel(tc, x, mus, log_vars, weights, out):
         def first_matmul(c, r):
             if r == 0:
                 gc_tiles[c] = stream.tile([P, ROWS * COMPS], BF16, name="gc", align_bytes=64)
-            c_ps = psum_c.tile([P, PACK, P], F32, name="c_ps")
+                cc_tiles[c] = stream.tile([P, ROWS * P], U32, name="cc", align_bytes=64)
+                cs_tiles[c] = stream.tile([P, ROWS * P], U8, name="cs", align_bytes=64)
+            c_ps = psum_c.tile([P, PACK, P], F32, name="c_ps", tag="c_ps")
             for t in range(PACK):
                 for g in range(PASSES):
                     w_cols = slice((t * PASSES + g) * P, (t * PASSES + g + 1) * P)
@@ -210,40 +216,35 @@ def tile_gaussianlayer_t_kernel(tc, x, mus, log_vars, weights, out):
                 op=ALU.mult,
             )
 
-        def quantise_c(c):
-            cc = stream.tile([P, ROWS * P], U32, name="cc", align_bytes=64)
-            cs = stream.tile([P, ROWS * P], U8, name="cs", align_bytes=64)
-            nc.vector.quantize_mx(out=cc[:].bitcast(FP8X4), scales=cs[:], in_=gc_tiles[c][:])
-            cc_tiles[c], cs_tiles[c] = cc, cs
+        def quantise_c(c, h):
+            words = slice(h * HALF_ROWS * P, (h + 1) * HALF_ROWS * P)
+            values = slice(h * HALF_ROWS * COMPS, (h + 1) * HALF_ROWS * COMPS)
+            nc.vector.quantize_mx(
+                out=cc_tiles[c][:, words].bitcast(FP8X4), scales=cs_tiles[c][:, words], in_=gc_tiles[c][:, values]
+            )
 
-        def second_matmul(c):
-            o_banks[c] = []
-            for h in range(ROWS // 2):
-                o_ps = psum_o.tile([P, 2 * OUT], F32, name="o_ps", tag="o_ps")
-                for s in range(2):
-                    b_cols = slice((2 * h + s) * P, (2 * h + s + 1) * P)
-                    nc.tensor.matmul_mx(
-                        out=o_ps[:, s * OUT : (s + 1) * OUT],
-                        lhsT=cc_tiles[c][:, b_cols].bitcast(FP8X4),
-                        lhsT_scale=cs_tiles[c][:, b_cols],
-                        rhs=gout_c[:].bitcast(FP8X4),
-                        rhs_scale=gout_s[:],
-                        start=True,
-                        stop=True,
-                    )
-                o_banks[c].append(o_ps)
-
-        def store_chunk(c):
-            o_sb = stream.tile([P, ROWS * OUT], F32, name="o_sb")
-            for h, o_ps in enumerate(o_banks[c]):
-                nc.scalar.activation(
-                    out=o_sb[:, 2 * h * OUT : 2 * (h + 1) * OUT], in_=o_ps[:], func=ACT.Copy,
-                    scale=inv_divisor[:, 0:1],
+        def second_matmul(c, h):
+            o_ps = psum_o.tile([P, HALF_ROWS * OUT], F32, name="o_ps", tag="o_ps")
+            for s in range(HALF_ROWS):
+                r = h * HALF_ROWS + s
+                nc.tensor.matmul_mx(
+                    out=o_ps[:, s * OUT : (s + 1) * OUT],
+                    lhsT=cc_tiles[c][:, r * P : (r + 1) * P].bitcast(FP8X4),
+                    lhsT_scale=cs_tiles[c][:, r * P : (r + 1) * P],
+                    rhs=gout_c[:].bitcast(FP8X4),
+                    rhs_scale=gout_s[:],
+                    start=True,
+                    stop=True,
                 )
-            rows = out[c * CHUNK : (c + 1) * CHUNK, :]
-            nc.sync.dma_start(out=rows.rearrange("(p r) j -> p (r j)", r=ROWS), in_=o_sb[:])
+            o_banks[(c, h)] = o_ps
 
-        transpose_chunk(0)
+        def store_half(c, h):
+            o_sb = stream.tile([P, HALF_ROWS * OUT], F32, name="o_sb", bufs=4)
+            nc.scalar.activation(out=o_sb[:], in_=o_banks[(c, h)][:], func=ACT.Copy, scale=inv_divisor[:, 0:1])
+            rows = out[c * CHUNK : (c + 1) * CHUNK, :].rearrange("(p h r) j -> p h (r j)", h=HALVES, r=HALF_ROWS)
+            nc.sync.dma_start(out=rows[:, h, :], in_=o_sb[:])
+
+        transpose_chunk(0, nc.vector.tensor_copy)
         quantise_x(0)
 
         gg_in = keep.tile([P, PACK * PASSES * P * PACK], BF16, name="gg_in", align_bytes=64)
@@ -256,20 +257,17 @@ def tile_gaussianlayer_t_kernel(tc, x, mus, log_vars, weights, out):
                 out=g_t[:], in_=sq_in[t][:], func=ACT.Exp, bias=log_norm[:, col : col + 1],
                 scale=neg_steep[:, col : col + 1],
             )
-            g_ps = psum_x.tile([P, PASSES * PACK, P], BF16, name="g_ps", tag="xt")
+            g_ps = psum_c.tile([P, PASSES * PACK, P], BF16, name="g_ps", tag="c_ps")
             for j in range(PASSES * PACK):
                 nc.tensor.transpose(g_ps[:, j, :], g_t[:, j * P : (j + 1) * P], ident_bf[:])
             nc.vector.tensor_copy(
                 out=gg_in[:, t * IN : (t + 1) * IN].rearrange("p (g m k) -> p g m k", g=PASSES, k=PACK),
                 in_=g_ps[:].rearrange("p (g k) m -> p g m k", k=PACK),
             )
-            words = slice(t * PASSES * P, (t + 1) * PASSES * P)
-            nc.vector.quantize_mx(
-                out=gin_c[:, words].bitcast(FP8X4), scales=gin_s[:, words], in_=gg_in[:, t * IN : (t + 1) * IN]
-            )
+        nc.vector.quantize_mx(out=gin_c[:].bitcast(FP8X4), scales=gin_s[:], in_=gg_in[:])
 
         for c in range(1, LOOKAHEAD):
-            transpose_chunk(c)
+            transpose_chunk(c, nc.scalar.copy)
             quantise_x(c)
 
         planes = keep.tile([P, PACK, OUT], BF16, name="planes")
@@ -295,23 +293,27 @@ def tile_gaussianlayer_t_kernel(tc, x, mus, log_vars, weights, out):
                 out=gout_c[:].bitcast(FP8X4), scales=gout_s[:], in_=gg_out[:].rearrange("p j t -> p (j t)")
             )
 
-        for i in range(N_CHUNKS + 2):
+        for i in range(N_CHUNKS + 1):
             if i + X_BUFS < N_CHUNKS:
                 load_chunk(i + X_BUFS)
-            if i + LOOKAHEAD < N_CHUNKS:
-                transpose_chunk(i + LOOKAHEAD)
-            if i >= 2:
-                store_chunk(i - 2)
             if i < N_CHUNKS:
                 for r in range(ROWS):
                     first_matmul(i, r)
                     if r == 0 and i >= 1:
-                        quantise_c(i - 1)
-                    if r == 2 and i + LOOKAHEAD < N_CHUNKS:
-                        quantise_x(i + LOOKAHEAD)
+                        quantise_c(i - 1, 1)
+                    if r == 1 and LOOKAHEAD <= i - 1 + LOOKAHEAD < N_CHUNKS:
+                        quantise_x(i - 1 + LOOKAHEAD)
+                    if r == 2:
+                        quantise_c(i, 0)
                 if i == 0:
                     make_g_out()
-            if i == N_CHUNKS:
-                quantise_c(i - 1)
-            if 1 <= i <= N_CHUNKS:
-                second_matmul(i - 1)
+            else:
+                quantise_c(i - 1, 1)
+            if i >= 1:
+                for h in range(HALVES):
+                    second_matmul(i - 1, h)
+            if i + LOOKAHEAD < N_CHUNKS:
+                transpose_chunk(i + LOOKAHEAD, nc.scalar.copy)
+            if i >= 1:
+                for h in range(HALVES):
+                    store_half(i - 1, h)

@@ -47,9 +47,9 @@ def tile_gaussianlayer_t_kernel(tc, x, mus, log_vars, weights, out):
         keep = ctx.enter_context(tc.tile_pool(name="keep", bufs=1))
         x_pool = ctx.enter_context(tc.tile_pool(name="x_pool", bufs=X_BUFS))
         stream = ctx.enter_context(tc.tile_pool(name="stream", bufs=3))
-        psum_x = ctx.enter_context(tc.psum_pool(name="psum_x", bufs=3))
+        psum_x = ctx.enter_context(tc.psum_pool(name="psum_x", bufs=4))
         psum_c = ctx.enter_context(tc.psum_pool(name="psum_c", bufs=3))
-        psum_o = ctx.enter_context(tc.psum_pool(name="psum_o", bufs=2))
+        psum_o = ctx.enter_context(tc.psum_pool(name="psum_o", bufs=1))
         ctx.enter_context(tc.manual_schedule())
 
         mus_sb = keep.tile([P, PACK * 2], BF16, name="mus_sb")
@@ -301,6 +301,8 @@ def tile_gaussianlayer_t_kernel(tc, x, mus, log_vars, weights, out):
                     first_matmul(i, r)
                     if r == 0 and i >= 1:
                         quantise_c(i - 1, 1)
+                        second_matmul(i - 1, 0)
+                        store_half(i - 1, 0)
                     if r == 1 and LOOKAHEAD <= i - 1 + LOOKAHEAD < N_CHUNKS:
                         quantise_x(i - 1 + LOOKAHEAD)
                     if r == 2:
@@ -308,12 +310,11 @@ def tile_gaussianlayer_t_kernel(tc, x, mus, log_vars, weights, out):
                 if i == 0:
                     make_g_out()
             else:
+                second_matmul(i - 1, 0)
+                store_half(i - 1, 0)
                 quantise_c(i - 1, 1)
             if i >= 1:
-                for h in range(HALVES):
-                    second_matmul(i - 1, h)
+                second_matmul(i - 1, 1)
+                store_half(i - 1, 1)
             if i + LOOKAHEAD < N_CHUNKS:
                 transpose_chunk(i + LOOKAHEAD, nc.scalar.copy)
-            if i >= 1:
-                for h in range(HALVES):
-                    store_half(i - 1, h)

@@ -6,7 +6,6 @@ from concourse.masks import make_identity
 
 F32 = mybir.dt.float32
 BF16 = mybir.dt.bfloat16
-I32 = mybir.dt.int32
 U32 = mybir.dt.uint32
 U8 = mybir.dt.uint8
 FP8X4 = mybir.dt.float8_e4m3fn_x4
@@ -19,26 +18,17 @@ FLOPS = 2 * BATCH * IN * COMPS + 2 * BATCH * COMPS * OUT
 P = 128
 PACK = 4
 K_PASS = P * PACK
+HALF_IN = IN // 2
 PASSES = IN // K_PASS
 ROWS = 4
 HALVES = 2
 HALF_ROWS = ROWS // HALVES
 CHUNK = ROWS * P
 N_CHUNKS = BATCH // CHUNK
-X_BUFS = 12
+X_BUFS = 8
+PRELOAD = 6
+MIDDLE = 0.5 * (IN - 1)
 LOOKAHEAD = 2
-
-ROUND_AND_BIAS = 1.5 * 2.0**23 + 127.0
-LN2_HI = 0.693145751953125
-LN2_LO = math.log(2.0) - LN2_HI
-EXP_DEGREE = 8
-
-
-def factorial(n):
-    product = 1
-    for factor in range(2, n + 1):
-        product *= factor
-    return product
 
 
 def tile_gaussianlayer_t_kernel(tc, x, mus, log_vars, weights, out):
@@ -56,26 +46,33 @@ def tile_gaussianlayer_t_kernel(tc, x, mus, log_vars, weights, out):
         nc.sync.dma_start(out=mus_sb[:], in_=mus.rearrange("(p t) c -> p (t c)", t=PACK))
         lv_sb = keep.tile([P, PACK * 2], BF16, name="lv_sb")
         nc.sync.dma_start(out=lv_sb[:], in_=log_vars.rearrange("(p t) c -> p (t c)", t=PACK))
+
         w_sb = keep.tile([P, PACK], BF16, name="w_sb")
         nc.sync.dma_start(out=w_sb[:], in_=weights.rearrange("(p t) -> p t", t=PACK))
 
         x_tiles = {}
 
-        def load_chunk(c):
+        def load_chunk(c, pieces=1):
             x_sb = x_pool.tile([P, ROWS * IN], BF16, name="x_sb")
-            rows = x[c * CHUNK : (c + 1) * CHUNK, :]
-            nc.sync.dma_start(out=x_sb[:], in_=rows.rearrange("(p r) k -> p (r k)", r=ROWS))
+            rows = x[c * CHUNK : (c + 1) * CHUNK, :].rearrange("(p r) k -> p (r k)", r=ROWS)
+            width = ROWS * IN // pieces
+            for piece in range(pieces):
+                cols = slice(piece * width, (piece + 1) * width)
+                nc.sync.dma_start(out=x_sb[:, cols], in_=rows[:, cols])
             x_tiles[c] = x_sb
 
-        for c in range(X_BUFS):
+        load_chunk(0, pieces=2)
+        for c in range(1, PRELOAD):
             load_chunk(c)
 
-        ones_bf = keep.tile([P, P], BF16, name="ones_bf")
-        nc.vector.memset(ones_bf[:], 1.0)
         warm = keep.tile([P, 1], F32, name="warm")
         nc.vector.memset(warm[:], 0.0)
         warm_out = keep.tile([P, 1], F32, name="warm_out")
         nc.scalar.activation(out=warm_out[:], in_=warm[:], func=ACT.Exp)
+        twos = keep.tile([P, PACK], F32, name="twos")
+        nc.vector.memset(twos[:], 2.0)
+        ones_bf = keep.tile([P, P], BF16, name="ones_bf")
+        nc.vector.memset(ones_bf[:], 1.0)
         k_row = keep.tile([P, IN], F32, name="k_row")
         nc.gpsimd.iota(
             k_row[:, 0 : 2 * P], pattern=[[1, 2], [2, P]], base=0, channel_multiplier=0,
@@ -89,100 +86,110 @@ def tile_gaussianlayer_t_kernel(tc, x, mus, log_vars, weights, out):
         ident_f32 = keep.tile([P, P], F32, name="ident_f32")
         make_identity(nc, ident_f32[:])
         ident_bf = keep.tile([P, P], BF16, name="ident_bf")
-        make_identity(nc, ident_bf[:])
+        nc.vector.tensor_copy(out=ident_bf[:], in_=ident_f32[:])
+        mid_row = keep.tile([P, IN], F32, name="mid_row")
+        nc.vector.tensor_scalar(out=mid_row[:], in0=k_row[:], scalar1=-MIDDLE, scalar2=None, op0=ALU.add)
 
         def by_axis(tile_ap, axis):
             return tile_ap.rearrange("p (t a) -> p t a", a=2)[:, :, axis]
 
         spans = (IN - 1, OUT - 1)
-        neg_centre = keep.tile([P, PACK * 2], F32, name="neg_centre")
+        neg_centre, neg_steep, log_norm = [], [], []
         for axis, span in enumerate(spans):
+            centre = keep.tile([P, PACK], F32, name="centre%d" % axis)
             nc.vector.tensor_scalar(
-                out=by_axis(neg_centre[:], axis), in0=by_axis(mus_sb[:], axis),
-                scalar1=-float(span), scalar2=None, op0=ALU.mult,
+                out=centre[:], in0=by_axis(mus_sb[:], axis), scalar1=-float(span), scalar2=None, op0=ALU.mult
             )
+            neg_centre.append(centre)
+        neg_twice = keep.tile([P, PACK], F32, name="neg_twice")
+        nc.vector.tensor_scalar(
+            out=neg_twice[:], in0=by_axis(mus_sb[:], 0), scalar1=-2.0 * (IN - 1), scalar2=2.0 * MIDDLE,
+            op0=ALU.mult, op1=ALU.add,
+        )
+        mid_centre = keep.tile([P, PACK], F32, name="mid_centre")
+        nc.vector.tensor_scalar(
+            out=mid_centre[:], in0=by_axis(mus_sb[:], 0), scalar1=-float(IN - 1), scalar2=MIDDLE,
+            op0=ALU.mult, op1=ALU.add,
+        )
 
-        sq_in = []
+        for axis, span in enumerate(spans):
+            power = keep.tile([P, PACK], F32, name="power%d" % axis)
+            nc.gpsimd.tensor_scalar(
+                out=power[:], in0=by_axis(lv_sb[:], axis), scalar1=-1.0 / math.log(2.0), scalar2=0.0,
+                op0=ALU.mult, op1=ALU.add,
+            )
+            raised = keep.tile([P, PACK], F32, name="raised%d" % axis)
+            nc.gpsimd.tensor_tensor(out=raised[:], in0=twos[:], in1=power[:], op=ALU.pow)
+            steep = keep.tile([P, PACK], F32, name="steep%d" % axis)
+            nc.gpsimd.tensor_scalar(
+                out=steep[:], in0=raised[:], scalar1=-0.5 / float(span * span), scalar2=0.0,
+                op0=ALU.mult, op1=ALU.add,
+            )
+            neg_steep.append(steep)
+            norm = keep.tile([P, PACK], F32, name="norm%d" % axis)
+            nc.vector.tensor_scalar(
+                out=norm[:], in0=by_axis(lv_sb[:], axis), scalar1=-0.5, scalar2=-0.5 * math.log(2.0 * math.pi),
+                op0=ALU.mult, op1=ALU.add,
+            )
+            log_norm.append(norm)
+
+        sq_in, bias_in = {}, {}
         for t in range(PACK):
-            sq = keep.tile([P, IN], F32, name="sq%d" % t)
+            sq_in[t] = keep.tile([P, IN], F32, name="sq%d" % t)
+            bias_in[t] = log_norm[0][:, t : t + 1]
+        for t in (0, 1):
             nc.scalar.activation(
-                out=sq[:], in_=k_row[:], func=ACT.Square, bias=neg_centre[:, 2 * t : 2 * t + 1], scale=1.0
+                out=sq_in[t][:], in_=k_row[:], func=ACT.Square, bias=neg_centre[0][:, t : t + 1], scale=1.0
             )
-            sq_in.append(sq)
-
-        shifted = keep.tile([P, PACK * 2], F32, name="shifted")
-        nc.vector.tensor_scalar(
-            out=shifted[:], in0=lv_sb[:], scalar1=-1.0 / math.log(2.0), scalar2=ROUND_AND_BIAS,
-            op0=ALU.mult, op1=ALU.add,
-        )
-        n_f32 = keep.tile([P, PACK * 2], F32, name="n_f32")
-        nc.vector.tensor_scalar(out=n_f32[:], in0=shifted[:], scalar1=ROUND_AND_BIAS, scalar2=None, op0=ALU.subtract)
-        rem = keep.tile([P, PACK * 2], F32, name="rem")
         nc.vector.scalar_tensor_tensor(
-            out=rem[:], in0=n_f32[:], scalar=-LN2_HI, in1=lv_sb[:], op0=ALU.mult, op1=ALU.subtract
+            out=sq_in[2][:], in0=mid_row[:], scalar=neg_twice[:, 2:3], in1=mid_row[:], op0=ALU.add, op1=ALU.mult
         )
-        nc.vector.scalar_tensor_tensor(
-            out=rem[:], in0=n_f32[:], scalar=-LN2_LO, in1=rem[:], op0=ALU.mult, op1=ALU.add
-        )
-        series = keep.tile([P, PACK * 2], F32, name="series")
-        nc.vector.tensor_scalar(
-            out=series[:], in0=rem[:], scalar1=1.0 / factorial(EXP_DEGREE), scalar2=None, op0=ALU.mult
-        )
-        for degree in range(EXP_DEGREE - 1, 0, -1):
-            nc.vector.scalar_tensor_tensor(
-                out=series[:], in0=series[:], scalar=1.0 / factorial(degree), in1=rem[:],
-                op0=ALU.add, op1=ALU.mult,
-            )
-        two_to_n = keep.tile([P, PACK * 2], I32, name="two_to_n")
-        nc.vector.tensor_single_scalar(
-            out=two_to_n[:], in_=shifted[:].bitcast(I32), scalar=23, op=ALU.logical_shift_left
-        )
-        scaled = keep.tile([P, PACK * 2], F32, name="scaled")
-        for axis, span in enumerate(spans):
-            nc.vector.tensor_scalar(
-                out=by_axis(scaled[:], axis), in0=by_axis(two_to_n[:].bitcast(F32), axis),
-                scalar1=-0.5 / float(span * span), scalar2=None, op0=ALU.mult,
-            )
-        neg_steep = keep.tile([P, PACK * 2], F32, name="neg_steep")
-        nc.vector.scalar_tensor_tensor(
-            out=neg_steep[:], in0=series[:], scalar=1.0, in1=scaled[:], op0=ALU.add, op1=ALU.mult
-        )
-        log_norm = keep.tile([P, PACK * 2], F32, name="log_norm")
-        nc.vector.tensor_scalar(
-            out=log_norm[:], in0=lv_sb[:], scalar1=-0.5, scalar2=-0.5 * math.log(2.0 * math.pi),
-            op0=ALU.mult, op1=ALU.add,
-        )
+        lift = keep.tile([P, 1], F32, name="lift")
+        nc.vector.tensor_tensor(out=lift[:], in0=mid_centre[:, 2:3], in1=mid_centre[:, 2:3], op=ALU.mult)
         w_f32 = keep.tile([P, PACK], F32, name="w_f32")
         nc.vector.tensor_copy(out=w_f32[:], in_=w_sb[:])
+        lifted = keep.tile([P, 1], F32, name="lifted")
+        nc.vector.scalar_tensor_tensor(
+            out=lifted[:], in0=lift[:], scalar=neg_steep[0][:, 2:3], in1=log_norm[0][:, 2:3], op0=ALU.mult, op1=ALU.add
+        )
+        bias_in[2] = lifted[:]
+        diff = keep.tile([P, IN], F32, name="diff")
+        nc.gpsimd.tensor_scalar(
+            out=diff[:], in0=k_row[:], scalar1=1.0, scalar2=neg_centre[0][:, 3:4], op0=ALU.mult, op1=ALU.add
+        )
+        nc.gpsimd.tensor_tensor(out=sq_in[3][:], in0=diff[:], in1=diff[:], op=ALU.mult)
+        sq_out = []
+        for t in range(PACK):
+            diff_o = keep.tile([P, OUT], F32, name="diff_o%d" % t)
+            nc.gpsimd.tensor_scalar(
+                out=diff_o[:].rearrange("p (s e) -> p s e", e=2),
+                in0=k_row[:, 0:OUT].rearrange("p (e s) -> p s e", e=2),
+                scalar1=1.0, scalar2=neg_centre[1][:, t : t + 1], op0=ALU.mult, op1=ALU.add,
+            )
+            sq_o = keep.tile([P, OUT], F32, name="sq_o%d" % t)
+            nc.gpsimd.tensor_tensor(out=sq_o[:], in0=diff_o[:], in1=diff_o[:], op=ALU.mult)
+            sq_out.append(sq_o)
 
-        w_ps = psum_o.tile([P, HALF_ROWS * OUT], F32, name="w_ps", tag="o_ps")
-        nc.tensor.matmul(out=w_ps[:, 0:PACK], lhsT=ones_bf[:], rhs=w_sb[:], start=True, stop=True)
-        w_sum = keep.tile([P, 1], F32, name="w_sum")
-        nc.vector.reduce_sum(out=w_sum[:], in_=w_ps[:, 0:PACK], axis=mybir.AxisListType.X)
-        divisor = keep.tile([P, 1], F32, name="divisor")
-        nc.vector.tensor_scalar(out=divisor[:], in0=w_sum[:], scalar1=float(IN), scalar2=None, op0=ALU.mult)
-        inv_divisor = keep.tile([P, 1], F32, name="inv_divisor")
-        nc.vector.reciprocal(out=inv_divisor[:], in_=divisor[:])
-
-        gx_tiles, xc_tiles, xs_tiles = {}, {}, {}
+        xt_banks, gx_tiles, xc_tiles, xs_tiles = {}, {}, {}, {}
         gc_tiles, cc_tiles, cs_tiles = {}, {}, {}
-        o_banks = {}
+        c_banks, o_banks = {}, {}
 
-        def transpose_chunk(c, copy_out):
+        def transpose_rows(c, r):
             words = x_tiles[c][:].bitcast(F32)
-            gx = stream.tile([P, ROWS * IN], BF16, name="gx", align_bytes=64)
-            gx_words = gx[:].bitcast(F32)
-            half = IN // 2
-            for r in range(ROWS):
-                xt = psum_x.tile([P, PACK, P], F32, name="xt")
-                for q in range(PACK):
-                    first = r * half + q * P
-                    nc.tensor.transpose(xt[:, q, :], words[:, first : first + P], ident_f32[:])
-                copy_out(
-                    out=gx_words[:, r * half : (r + 1) * half].rearrange("p (g b u) -> p g b u", g=PASSES, u=2),
-                    in_=xt[:].rearrange("p (g u) b -> p g b u", u=2),
-                )
-            gx_tiles[c] = gx
+            xt = psum_x.tile([P, PACK, P], F32, name="xt")
+            for q in range(PACK):
+                first = r * HALF_IN + q * P
+                nc.tensor.transpose(xt[:, q, :], words[:, first : first + P], ident_f32[:])
+            xt_banks[(c, r)] = xt
+
+        def copy_rows(c, r, copy_out):
+            if r == 0:
+                gx_tiles[c] = stream.tile([P, ROWS * IN], BF16, name="gx", align_bytes=64)
+            gx_words = gx_tiles[c][:].bitcast(F32)
+            copy_out(
+                out=gx_words[:, r * HALF_IN : (r + 1) * HALF_IN].rearrange("p (g b u) -> p g b u", g=PASSES, u=2),
+                in_=xt_banks[(c, r)][:].rearrange("p (g u) b -> p g b u", u=2),
+            )
 
         def quantise_x(c):
             xc = stream.tile([P, ROWS * PASSES * P], U32, name="xc", align_bytes=64, bufs=LOOKAHEAD + 2)
@@ -190,28 +197,28 @@ def tile_gaussianlayer_t_kernel(tc, x, mus, log_vars, weights, out):
             nc.vector.quantize_mx(out=xc[:].bitcast(FP8X4), scales=xs[:], in_=gx_tiles[c][:])
             xc_tiles[c], xs_tiles[c] = xc, xs
 
-        def first_matmul(c, r):
+        def first_matmul(c, r, t):
+            for g in range(PASSES):
+                w_cols = slice((t * PASSES + g) * P, (t * PASSES + g + 1) * P)
+                x_cols = slice((r * PASSES + g) * P, (r * PASSES + g + 1) * P)
+                nc.tensor.matmul_mx(
+                    out=c_banks[(c, r)][:, t, :],
+                    lhsT=gin_c[:, w_cols].bitcast(FP8X4),
+                    lhsT_scale=gin_s[:, w_cols],
+                    rhs=xc_tiles[c][:, x_cols].bitcast(FP8X4),
+                    rhs_scale=xs_tiles[c][:, x_cols],
+                    start=(g == 0),
+                    stop=(g == PASSES - 1),
+                )
+
+        def weigh(c, r):
             if r == 0:
                 gc_tiles[c] = stream.tile([P, ROWS * COMPS], BF16, name="gc", align_bytes=64)
                 cc_tiles[c] = stream.tile([P, ROWS * P], U32, name="cc", align_bytes=64)
                 cs_tiles[c] = stream.tile([P, ROWS * P], U8, name="cs", align_bytes=64)
-            c_ps = psum_c.tile([P, PACK, P], F32, name="c_ps", tag="c_ps")
-            for t in range(PACK):
-                for g in range(PASSES):
-                    w_cols = slice((t * PASSES + g) * P, (t * PASSES + g + 1) * P)
-                    x_cols = slice((r * PASSES + g) * P, (r * PASSES + g + 1) * P)
-                    nc.tensor.matmul_mx(
-                        out=c_ps[:, t, :],
-                        lhsT=gin_c[:, w_cols].bitcast(FP8X4),
-                        lhsT_scale=gin_s[:, w_cols],
-                        rhs=xc_tiles[c][:, x_cols].bitcast(FP8X4),
-                        rhs_scale=xs_tiles[c][:, x_cols],
-                        start=(g == 0),
-                        stop=(g == PASSES - 1),
-                    )
             nc.vector.tensor_tensor(
                 out=gc_tiles[c][:, r * COMPS : (r + 1) * COMPS].rearrange("p (b t) -> p b t", t=PACK),
-                in0=c_ps[:].rearrange("p t b -> p b t"),
+                in0=c_banks[(c, r)][:].rearrange("p t b -> p b t"),
                 in1=w_f32[:].unsqueeze(1).to_broadcast([P, P, PACK]),
                 op=ALU.mult,
             )
@@ -244,77 +251,128 @@ def tile_gaussianlayer_t_kernel(tc, x, mus, log_vars, weights, out):
             rows = out[c * CHUNK : (c + 1) * CHUNK, :].rearrange("(p h r) j -> p h (r j)", h=HALVES, r=HALF_ROWS)
             nc.sync.dma_start(out=rows[:, h, :], in_=o_sb[:])
 
-        transpose_chunk(0, nc.vector.tensor_copy)
-        quantise_x(0)
-
         gg_in = keep.tile([P, PACK * PASSES * P * PACK], BF16, name="gg_in", align_bytes=64)
         gin_c = keep.tile([P, PACK * PASSES * P], U32, name="gin_c", align_bytes=64)
         gin_s = keep.tile([P, PACK * PASSES * P], U8, name="gin_s", align_bytes=64)
-        for t in range(PACK):
-            col = 2 * t
+        g_rows, g_banks = {}, {}
+
+        def gauss_in(t):
             g_t = stream.tile([P, IN], BF16, name="g_t", bufs=2)
             nc.scalar.activation(
-                out=g_t[:], in_=sq_in[t][:], func=ACT.Exp, bias=log_norm[:, col : col + 1],
-                scale=neg_steep[:, col : col + 1],
+                out=g_t[:], in_=sq_in[t][:], func=ACT.Exp, bias=bias_in[t], scale=neg_steep[0][:, t : t + 1]
             )
-            g_ps = psum_c.tile([P, PASSES * PACK, P], BF16, name="g_ps", tag="c_ps")
-            for j in range(PASSES * PACK):
-                nc.tensor.transpose(g_ps[:, j, :], g_t[:, j * P : (j + 1) * P], ident_bf[:])
-            nc.vector.tensor_copy(
-                out=gg_in[:, t * IN : (t + 1) * IN].rearrange("p (g m k) -> p g m k", g=PASSES, k=PACK),
-                in_=g_ps[:].rearrange("p (g k) m -> p g m k", k=PACK),
-            )
-        nc.vector.quantize_mx(out=gin_c[:].bitcast(FP8X4), scales=gin_s[:], in_=gg_in[:])
+            g_rows[t] = g_t
 
-        for c in range(1, LOOKAHEAD):
-            transpose_chunk(c, nc.scalar.copy)
-            quantise_x(c)
+        def transpose_gauss(t):
+            if t < 3:
+                g_ps = psum_c.tile([P, PASSES * PACK, P], BF16, name="g_ps", tag="c_ps")
+            else:
+                g_ps = psum_o.tile([P, PASSES * PACK, P], BF16, name="g_po", tag="o_ps")
+            for j in range(PASSES * PACK):
+                nc.tensor.transpose(g_ps[:, j, :], g_rows[t][:, j * P : (j + 1) * P], ident_bf[:])
+            g_banks[t] = g_ps
+
+        def copy_gauss(t, copy_out):
+            copy_out(
+                out=gg_in[:, t * IN : (t + 1) * IN].rearrange("p (g m k) -> p g m k", g=PASSES, k=PACK),
+                in_=g_banks[t][:].rearrange("p (g k) m -> p g m k", k=PACK),
+            )
+
+        def quantise_gauss(t):
+            words = slice(t * PASSES * P, (t + 1) * PASSES * P)
+            nc.vector.quantize_mx(
+                out=gin_c[:, words].bitcast(FP8X4), scales=gin_s[:, words], in_=gg_in[:, t * IN : (t + 1) * IN]
+            )
+
+        for r in range(ROWS):
+            transpose_rows(0, r)
+            copy_rows(0, r, nc.vector.tensor_copy)
+        w_ps = psum_o.tile([P, HALF_ROWS * OUT], F32, name="w_ps", tag="o_ps")
+        nc.tensor.matmul(out=w_ps[:, 0:PACK], lhsT=ones_bf[:], rhs=w_sb[:], start=True, stop=True)
+        w_sum = keep.tile([P, 1], F32, name="w_sum")
+        nc.vector.reduce_sum(out=w_sum[:], in_=w_ps[:, 0:PACK], axis=mybir.AxisListType.X)
+        for t in range(PACK):
+            gauss_in(t)
+            transpose_gauss(t)
+            transpose_rows(1, t)
+        quantise_x(0)
+        copy_gauss(0, nc.vector.tensor_copy)
+        copy_gauss(1, nc.vector.tensor_copy)
+        quantise_gauss(0)
+        copy_gauss(2, nc.vector.tensor_copy)
+        quantise_gauss(1)
+        copy_gauss(3, nc.scalar.copy)
+        quantise_gauss(2)
+        quantise_gauss(3)
+        for r in range(ROWS):
+            copy_rows(1, r, nc.scalar.copy if r < 2 else nc.vector.tensor_copy)
+        divisor = keep.tile([P, 1], F32, name="divisor")
+        nc.vector.tensor_scalar(out=divisor[:], in0=w_sum[:], scalar1=float(IN), scalar2=None, op0=ALU.mult)
+        inv_divisor = keep.tile([P, 1], F32, name="inv_divisor")
+        nc.vector.reciprocal(out=inv_divisor[:], in_=divisor[:])
+
+
+        for r in range(ROWS):
+            pool, tag = (psum_c, "c_ps") if r < 3 else (psum_o, "o_ps")
+            c_ps = pool.tile([P, PACK, P], F32, name="c_ps", tag=tag)
+            c_banks[(0, r)] = c_ps
+        for step in range(PACK):
+            for t in range(step):
+                first_matmul(0, step, t)
+            for r in range(step + 1):
+                first_matmul(0, r, step)
+        quantise_x(1)
+        weigh(0, 0)
+        weigh(0, 1)
+        weigh(0, 2)
+        quantise_c(0, 0)
+        weigh(0, 3)
 
         planes = keep.tile([P, PACK, OUT], BF16, name="planes")
         gg_out = keep.tile([P, OUT, PACK], BF16, name="gg_out", align_bytes=64)
         gout_c = keep.tile([P, OUT], U32, name="gout_c", align_bytes=64)
         gout_s = keep.tile([P, OUT], U8, name="gout_s", align_bytes=64)
-
-        def make_g_out():
-            for t in range(PACK):
-                col = 2 * t + 1
-                sq_o = stream.tile([P, OUT], F32, name="sq_o", bufs=2)
-                nc.scalar.activation(
-                    out=sq_o[:].rearrange("p (s e) -> p s e", e=2),
-                    in_=k_row[:, 0:OUT].rearrange("p (e s) -> p s e", e=2),
-                    func=ACT.Square, bias=neg_centre[:, col : col + 1], scale=1.0,
-                )
-                nc.scalar.activation(
-                    out=planes[:, t, :], in_=sq_o[:], func=ACT.Exp, bias=log_norm[:, col : col + 1],
-                    scale=neg_steep[:, col : col + 1],
-                )
-            nc.vector.tensor_copy(out=gg_out[:], in_=planes[:].rearrange("p t j -> p j t"))
-            nc.vector.quantize_mx(
-                out=gout_c[:].bitcast(FP8X4), scales=gout_s[:], in_=gg_out[:].rearrange("p j t -> p (j t)")
+        for t in range(PACK):
+            nc.scalar.activation(
+                out=planes[:, t, :], in_=sq_out[t][:], func=ACT.Exp, bias=log_norm[1][:, t : t + 1],
+                scale=neg_steep[1][:, t : t + 1],
             )
+        for r in range(ROWS):
+            transpose_rows(2, r)
+            copy_rows(2, r, nc.scalar.copy)
 
-        for i in range(N_CHUNKS + 1):
-            if i + X_BUFS < N_CHUNKS:
-                load_chunk(i + X_BUFS)
+        for i in range(1, N_CHUNKS + 1):
+            if i - 1 + PRELOAD < N_CHUNKS:
+                load_chunk(i - 1 + PRELOAD)
             if i < N_CHUNKS:
                 for r in range(ROWS):
-                    first_matmul(i, r)
-                    if r == 0 and i >= 1:
+                    c_ps = psum_c.tile([P, PACK, P], F32, name="c_ps", tag="c_ps")
+                    c_banks[(i, r)] = c_ps
+                    for t in range(PACK):
+                        first_matmul(i, r, t)
+                    weigh(i, r)
+                    if r == 0:
                         quantise_c(i - 1, 1)
+                        if i == 1:
+                            nc.vector.tensor_copy(out=gg_out[:], in_=planes[:].rearrange("p t j -> p j t"))
+                            nc.vector.quantize_mx(
+                                out=gout_c[:].bitcast(FP8X4), scales=gout_s[:],
+                                in_=gg_out[:].rearrange("p j t -> p (j t)"),
+                            )
+                    if r == (2 if i == 1 else 0):
                         second_matmul(i - 1, 0)
                         store_half(i - 1, 0)
-                    if r == 1 and LOOKAHEAD <= i - 1 + LOOKAHEAD < N_CHUNKS:
-                        quantise_x(i - 1 + LOOKAHEAD)
+                    if r == 1 and i + 1 < N_CHUNKS:
+                        quantise_x(i + 1)
                     if r == 2:
                         quantise_c(i, 0)
-                if i == 0:
-                    make_g_out()
             else:
                 second_matmul(i - 1, 0)
                 store_half(i - 1, 0)
                 quantise_c(i - 1, 1)
-            if i >= 1:
-                second_matmul(i - 1, 1)
-                store_half(i - 1, 1)
+            second_matmul(i - 1, 1)
+            store_half(i - 1, 1)
             if i + LOOKAHEAD < N_CHUNKS:
-                transpose_chunk(i + LOOKAHEAD, nc.scalar.copy)
+                for r in range(ROWS):
+                    transpose_rows(i + LOOKAHEAD, r)
+                    copy_rows(i + LOOKAHEAD, r, nc.scalar.copy)

@@ -18,6 +18,7 @@ FLOPS = 2 * BATCH * IN * COMPS + 2 * BATCH * COMPS * OUT
 P = 128
 PACK = 4
 K_PASS = P * PACK
+BANKS = 8
 HALF_IN = IN // 2
 PASSES = IN // K_PASS
 ROWS = 4
@@ -28,6 +29,7 @@ N_CHUNKS = BATCH // CHUNK
 X_BUFS = 8
 PRELOAD = 6
 MIDDLE = 0.5 * (IN - 1)
+VECTOR_FROM = 2
 LOOKAHEAD = 2
 
 
@@ -37,9 +39,7 @@ def tile_gaussianlayer_t_kernel(tc, x, mus, log_vars, weights, out):
         keep = ctx.enter_context(tc.tile_pool(name="keep", bufs=1))
         x_pool = ctx.enter_context(tc.tile_pool(name="x_pool", bufs=X_BUFS))
         stream = ctx.enter_context(tc.tile_pool(name="stream", bufs=3))
-        psum_x = ctx.enter_context(tc.psum_pool(name="psum_x", bufs=4))
-        psum_c = ctx.enter_context(tc.psum_pool(name="psum_c", bufs=3))
-        psum_o = ctx.enter_context(tc.psum_pool(name="psum_o", bufs=1))
+        psum = ctx.enter_context(tc.psum_pool(name="psum", bufs=BANKS))
         ctx.enter_context(tc.manual_schedule())
 
         mus_sb = keep.tile([P, PACK * 2], BF16, name="mus_sb")
@@ -137,38 +137,39 @@ def tile_gaussianlayer_t_kernel(tc, x, mus, log_vars, weights, out):
         for t in range(PACK):
             sq_in[t] = keep.tile([P, IN], F32, name="sq%d" % t)
             bias_in[t] = log_norm[0][:, t : t + 1]
-        for t in (0, 1):
+        for t in range(VECTOR_FROM):
             nc.scalar.activation(
                 out=sq_in[t][:], in_=k_row[:], func=ACT.Square, bias=neg_centre[0][:, t : t + 1], scale=1.0
             )
-        nc.vector.scalar_tensor_tensor(
-            out=sq_in[2][:], in0=mid_row[:], scalar=neg_twice[:, 2:3], in1=mid_row[:], op0=ALU.add, op1=ALU.mult
-        )
-        lift = keep.tile([P, 1], F32, name="lift")
-        nc.vector.tensor_tensor(out=lift[:], in0=mid_centre[:, 2:3], in1=mid_centre[:, 2:3], op=ALU.mult)
+        for t in range(VECTOR_FROM, PACK):
+            nc.vector.scalar_tensor_tensor(
+                out=sq_in[t][:], in0=mid_row[:], scalar=neg_twice[:, t : t + 1], in1=mid_row[:],
+                op0=ALU.add, op1=ALU.mult,
+            )
         w_f32 = keep.tile([P, PACK], F32, name="w_f32")
         nc.vector.tensor_copy(out=w_f32[:], in_=w_sb[:])
-        lifted = keep.tile([P, 1], F32, name="lifted")
-        nc.vector.scalar_tensor_tensor(
-            out=lifted[:], in0=lift[:], scalar=neg_steep[0][:, 2:3], in1=log_norm[0][:, 2:3], op0=ALU.mult, op1=ALU.add
-        )
-        bias_in[2] = lifted[:]
-        diff = keep.tile([P, IN], F32, name="diff")
-        nc.gpsimd.tensor_scalar(
-            out=diff[:], in0=k_row[:], scalar1=1.0, scalar2=neg_centre[0][:, 3:4], op0=ALU.mult, op1=ALU.add
-        )
-        nc.gpsimd.tensor_tensor(out=sq_in[3][:], in0=diff[:], in1=diff[:], op=ALU.mult)
+
+        def make_bias():
+            lift = keep.tile([P, PACK], F32, name="lift")
+            nc.vector.tensor_tensor(out=lift[:], in0=mid_centre[:], in1=mid_centre[:], op=ALU.mult)
+            lifted = keep.tile([P, PACK], F32, name="lifted")
+            nc.vector.tensor_tensor(out=lifted[:], in0=lift[:], in1=neg_steep[0][:], op=ALU.mult)
+            biased = keep.tile([P, PACK], F32, name="biased")
+            nc.vector.tensor_tensor(out=biased[:], in0=lifted[:], in1=log_norm[0][:], op=ALU.add)
+            for t in range(VECTOR_FROM, PACK):
+                bias_in[t] = biased[:, t : t + 1]
+
         sq_out = []
-        for t in range(PACK):
-            diff_o = keep.tile([P, OUT], F32, name="diff_o%d" % t)
-            nc.gpsimd.tensor_scalar(
-                out=diff_o[:].rearrange("p (s e) -> p s e", e=2),
-                in0=k_row[:, 0:OUT].rearrange("p (e s) -> p s e", e=2),
-                scalar1=1.0, scalar2=neg_centre[1][:, t : t + 1], op0=ALU.mult, op1=ALU.add,
-            )
-            sq_o = keep.tile([P, OUT], F32, name="sq_o%d" % t)
-            nc.gpsimd.tensor_tensor(out=sq_o[:], in0=diff_o[:], in1=diff_o[:], op=ALU.mult)
-            sq_out.append(sq_o)
+
+        def square_out():
+            for t in range(PACK):
+                sq_o = keep.tile([P, OUT], F32, name="sq_o%d" % t)
+                nc.scalar.activation(
+                    out=sq_o[:].rearrange("p (s e) -> p s e", e=2),
+                    in_=k_row[:, 0:OUT].rearrange("p (e s) -> p s e", e=2),
+                    func=ACT.Square, bias=neg_centre[1][:, t : t + 1], scale=1.0,
+                )
+                sq_out.append(sq_o)
 
         xt_banks, gx_tiles, xc_tiles, xs_tiles = {}, {}, {}, {}
         gc_tiles, cc_tiles, cs_tiles = {}, {}, {}
@@ -176,7 +177,7 @@ def tile_gaussianlayer_t_kernel(tc, x, mus, log_vars, weights, out):
 
         def transpose_rows(c, r):
             words = x_tiles[c][:].bitcast(F32)
-            xt = psum_x.tile([P, PACK, P], F32, name="xt")
+            xt = psum.tile([P, PACK, P], F32, name="xt", tag="bank")
             for q in range(PACK):
                 first = r * HALF_IN + q * P
                 nc.tensor.transpose(xt[:, q, :], words[:, first : first + P], ident_f32[:])
@@ -231,7 +232,7 @@ def tile_gaussianlayer_t_kernel(tc, x, mus, log_vars, weights, out):
             )
 
         def second_matmul(c, h):
-            o_ps = psum_o.tile([P, HALF_ROWS * OUT], F32, name="o_ps", tag="o_ps")
+            o_ps = psum.tile([P, HALF_ROWS * OUT], F32, name="o_ps", tag="bank")
             for s in range(HALF_ROWS):
                 r = h * HALF_ROWS + s
                 nc.tensor.matmul_mx(
@@ -264,13 +265,9 @@ def tile_gaussianlayer_t_kernel(tc, x, mus, log_vars, weights, out):
             g_rows[t] = g_t
 
         def transpose_gauss(t):
-            if t < 3:
-                g_ps = psum_c.tile([P, PASSES * PACK, P], BF16, name="g_ps", tag="c_ps")
-            else:
-                g_ps = psum_o.tile([P, PASSES * PACK, P], BF16, name="g_po", tag="o_ps")
+            g_ps = g_banks[t]
             for j in range(PASSES * PACK):
                 nc.tensor.transpose(g_ps[:, j, :], g_rows[t][:, j * P : (j + 1) * P], ident_bf[:])
-            g_banks[t] = g_ps
 
         def copy_gauss(t, copy_out):
             copy_out(
@@ -287,14 +284,20 @@ def tile_gaussianlayer_t_kernel(tc, x, mus, log_vars, weights, out):
         for r in range(ROWS):
             transpose_rows(0, r)
             copy_rows(0, r, nc.vector.tensor_copy)
-        w_ps = psum_o.tile([P, HALF_ROWS * OUT], F32, name="w_ps", tag="o_ps")
+            if r == 1:
+                make_bias()
+        w_ps = psum.tile([P, HALF_ROWS * OUT], F32, name="w_ps", tag="bank")
         nc.tensor.matmul(out=w_ps[:, 0:PACK], lhsT=ones_bf[:], rhs=w_sb[:], start=True, stop=True)
         w_sum = keep.tile([P, 1], F32, name="w_sum")
         nc.vector.reduce_sum(out=w_sum[:], in_=w_ps[:, 0:PACK], axis=mybir.AxisListType.X)
         for t in range(PACK):
+            g_ps = psum.tile([P, PASSES * PACK, P], BF16, name="g_ps", tag="bank")
+            g_banks[t] = g_ps
+        for t in range(PACK):
             gauss_in(t)
             transpose_gauss(t)
             transpose_rows(1, t)
+        square_out()
         quantise_x(0)
         copy_gauss(0, nc.vector.tensor_copy)
         copy_gauss(1, nc.vector.tensor_copy)
@@ -313,21 +316,13 @@ def tile_gaussianlayer_t_kernel(tc, x, mus, log_vars, weights, out):
 
 
         for r in range(ROWS):
-            pool, tag = (psum_c, "c_ps") if r < 3 else (psum_o, "o_ps")
-            c_ps = pool.tile([P, PACK, P], F32, name="c_ps", tag=tag)
+            c_ps = psum.tile([P, PACK, P], F32, name="c_ps", tag="bank")
             c_banks[(0, r)] = c_ps
         for step in range(PACK):
             for t in range(step):
                 first_matmul(0, step, t)
             for r in range(step + 1):
                 first_matmul(0, r, step)
-        quantise_x(1)
-        weigh(0, 0)
-        weigh(0, 1)
-        weigh(0, 2)
-        quantise_c(0, 0)
-        weigh(0, 3)
-
         planes = keep.tile([P, PACK, OUT], BF16, name="planes")
         gg_out = keep.tile([P, OUT, PACK], BF16, name="gg_out", align_bytes=64)
         gout_c = keep.tile([P, OUT], U32, name="gout_c", align_bytes=64)
@@ -337,6 +332,17 @@ def tile_gaussianlayer_t_kernel(tc, x, mus, log_vars, weights, out):
                 out=planes[:, t, :], in_=sq_out[t][:], func=ACT.Exp, bias=log_norm[1][:, t : t + 1],
                 scale=neg_steep[1][:, t : t + 1],
             )
+        quantise_x(1)
+        weigh(0, 0)
+        nc.vector.tensor_copy(out=gg_out[:], in_=planes[:].rearrange("p t j -> p j t"))
+        weigh(0, 1)
+        nc.vector.quantize_mx(
+            out=gout_c[:].bitcast(FP8X4), scales=gout_s[:], in_=gg_out[:].rearrange("p j t -> p (j t)")
+        )
+        weigh(0, 2)
+        quantise_c(0, 0)
+        weigh(0, 3)
+
         for r in range(ROWS):
             transpose_rows(2, r)
             copy_rows(2, r, nc.scalar.copy)
@@ -346,20 +352,14 @@ def tile_gaussianlayer_t_kernel(tc, x, mus, log_vars, weights, out):
                 load_chunk(i - 1 + PRELOAD)
             if i < N_CHUNKS:
                 for r in range(ROWS):
-                    c_ps = psum_c.tile([P, PACK, P], F32, name="c_ps", tag="c_ps")
+                    c_ps = psum.tile([P, PACK, P], F32, name="c_ps", tag="bank")
                     c_banks[(i, r)] = c_ps
                     for t in range(PACK):
                         first_matmul(i, r, t)
                     weigh(i, r)
                     if r == 0:
                         quantise_c(i - 1, 1)
-                        if i == 1:
-                            nc.vector.tensor_copy(out=gg_out[:], in_=planes[:].rearrange("p t j -> p j t"))
-                            nc.vector.quantize_mx(
-                                out=gout_c[:].bitcast(FP8X4), scales=gout_s[:],
-                                in_=gg_out[:].rearrange("p j t -> p (j t)"),
-                            )
-                    if r == (2 if i == 1 else 0):
+                    if r == 0:
                         second_matmul(i - 1, 0)
                         store_half(i - 1, 0)
                     if r == 1 and i + 1 < N_CHUNKS:

@@ -193,8 +193,8 @@ def tile_gaussianlayer_t_kernel(tc, x, mus, log_vars, weights, out):
             )
 
         def quantise_x(c):
-            xc = stream.tile([P, ROWS * PASSES * P], U32, name="xc", align_bytes=64, bufs=LOOKAHEAD + 2)
-            xs = stream.tile([P, ROWS * PASSES * P], U8, name="xs", align_bytes=64, bufs=LOOKAHEAD + 2)
+            xc = stream.tile([P, ROWS * PASSES * P], U32, name="xc", align_bytes=256, bufs=LOOKAHEAD + 2)
+            xs = stream.tile([P, ROWS * PASSES * P], U8, name="xs", align_bytes=256, bufs=LOOKAHEAD + 2)
             nc.vector.quantize_mx(out=xc[:].bitcast(FP8X4), scales=xs[:], in_=gx_tiles[c][:])
             xc_tiles[c], xs_tiles[c] = xc, xs
 
@@ -215,8 +215,8 @@ def tile_gaussianlayer_t_kernel(tc, x, mus, log_vars, weights, out):
         def weigh(c, r):
             if r == 0:
                 gc_tiles[c] = stream.tile([P, ROWS * COMPS], BF16, name="gc", align_bytes=64)
-                cc_tiles[c] = stream.tile([P, ROWS * P], U32, name="cc", align_bytes=64)
-                cs_tiles[c] = stream.tile([P, ROWS * P], U8, name="cs", align_bytes=64)
+                cc_tiles[c] = stream.tile([P, ROWS * P], U32, name="cc", align_bytes=256)
+                cs_tiles[c] = stream.tile([P, ROWS * P], U8, name="cs", align_bytes=256)
             nc.vector.tensor_tensor(
                 out=gc_tiles[c][:, r * COMPS : (r + 1) * COMPS].rearrange("p (b t) -> p b t", t=PACK),
                 in0=c_banks[(c, r)][:].rearrange("p t b -> p b t"),
@@ -224,17 +224,17 @@ def tile_gaussianlayer_t_kernel(tc, x, mus, log_vars, weights, out):
                 op=ALU.mult,
             )
 
-        def quantise_c(c, h):
-            words = slice(h * HALF_ROWS * P, (h + 1) * HALF_ROWS * P)
-            values = slice(h * HALF_ROWS * COMPS, (h + 1) * HALF_ROWS * COMPS)
+        def quantise_c(c, first, rows=HALF_ROWS):
+            words = slice(first * P, (first + rows) * P)
+            values = slice(first * COMPS, (first + rows) * COMPS)
             nc.vector.quantize_mx(
                 out=cc_tiles[c][:, words].bitcast(FP8X4), scales=cs_tiles[c][:, words], in_=gc_tiles[c][:, values]
             )
 
-        def second_matmul(c, h):
+        def second_matmul(c, first, rows=HALF_ROWS):
             o_ps = psum.tile([P, HALF_ROWS * OUT], F32, name="o_ps", tag="bank")
-            for s in range(HALF_ROWS):
-                r = h * HALF_ROWS + s
+            for s in range(rows):
+                r = first + s
                 nc.tensor.matmul_mx(
                     out=o_ps[:, s * OUT : (s + 1) * OUT],
                     lhsT=cc_tiles[c][:, r * P : (r + 1) * P].bitcast(FP8X4),
@@ -244,17 +244,24 @@ def tile_gaussianlayer_t_kernel(tc, x, mus, log_vars, weights, out):
                     start=True,
                     stop=True,
                 )
-            o_banks[(c, h)] = o_ps
+            o_banks[(c, first)] = o_ps
 
-        def store_half(c, h):
-            o_sb = stream.tile([P, HALF_ROWS * OUT], F32, name="o_sb", bufs=4)
-            nc.scalar.activation(out=o_sb[:], in_=o_banks[(c, h)][:], func=ACT.Copy, scale=inv_divisor[:, 0:1])
-            rows = out[c * CHUNK : (c + 1) * CHUNK, :].rearrange("(p h r) j -> p h (r j)", h=HALVES, r=HALF_ROWS)
-            nc.sync.dma_start(out=rows[:, h, :], in_=o_sb[:])
+        def store_rows(c, first, rows=HALF_ROWS, on_vector=False):
+            o_sb = stream.tile([P, HALF_ROWS * OUT], F32, name="o_sb", bufs=8)
+            cols = slice(0, rows * OUT)
+            bank = o_banks[(c, first)][:, cols]
+            if on_vector:
+                nc.vector.tensor_scalar(
+                    out=o_sb[:, cols], in0=bank, scalar1=inv_divisor[:, 0:1], scalar2=None, op0=ALU.mult
+                )
+            else:
+                nc.scalar.activation(out=o_sb[:, cols], in_=bank, func=ACT.Copy, scale=inv_divisor[:, 0:1])
+            chunk = out[c * CHUNK : (c + 1) * CHUNK, :].rearrange("(p r) j -> p (r j)", r=ROWS)
+            nc.sync.dma_start(out=chunk[:, first * OUT : (first + rows) * OUT], in_=o_sb[:, cols])
 
         gg_in = keep.tile([P, PACK * PASSES * P * PACK], BF16, name="gg_in", align_bytes=64)
-        gin_c = keep.tile([P, PACK * PASSES * P], U32, name="gin_c", align_bytes=64)
-        gin_s = keep.tile([P, PACK * PASSES * P], U8, name="gin_s", align_bytes=64)
+        gin_c = keep.tile([P, PACK * PASSES * P], U32, name="gin_c", align_bytes=256)
+        gin_s = keep.tile([P, PACK * PASSES * P], U8, name="gin_s", align_bytes=256)
         g_rows, g_banks = {}, {}
 
         def gauss_in(t):
@@ -325,8 +332,8 @@ def tile_gaussianlayer_t_kernel(tc, x, mus, log_vars, weights, out):
                 first_matmul(0, r, step)
         planes = keep.tile([P, PACK, OUT], BF16, name="planes")
         gg_out = keep.tile([P, OUT, PACK], BF16, name="gg_out", align_bytes=64)
-        gout_c = keep.tile([P, OUT], U32, name="gout_c", align_bytes=64)
-        gout_s = keep.tile([P, OUT], U8, name="gout_s", align_bytes=64)
+        gout_c = keep.tile([P, OUT], U32, name="gout_c", align_bytes=256)
+        gout_s = keep.tile([P, OUT], U8, name="gout_s", align_bytes=256)
         for t in range(PACK):
             nc.scalar.activation(
                 out=planes[:, t, :], in_=sq_out[t][:], func=ACT.Exp, bias=log_norm[1][:, t : t + 1],
@@ -347,32 +354,34 @@ def tile_gaussianlayer_t_kernel(tc, x, mus, log_vars, weights, out):
             transpose_rows(2, r)
             copy_rows(2, r, nc.scalar.copy)
 
-        for i in range(1, N_CHUNKS + 1):
+        for i in range(1, N_CHUNKS):
+            last = i == N_CHUNKS - 1
             if i - 1 + PRELOAD < N_CHUNKS:
                 load_chunk(i - 1 + PRELOAD)
-            if i < N_CHUNKS:
-                for r in range(ROWS):
-                    c_ps = psum.tile([P, PACK, P], F32, name="c_ps", tag="bank")
-                    c_banks[(i, r)] = c_ps
-                    for t in range(PACK):
-                        first_matmul(i, r, t)
-                    weigh(i, r)
-                    if r == 0:
-                        quantise_c(i - 1, 1)
-                    if r == 0:
-                        second_matmul(i - 1, 0)
-                        store_half(i - 1, 0)
-                    if r == 1 and i + 1 < N_CHUNKS:
-                        quantise_x(i + 1)
-                    if r == 2:
-                        quantise_c(i, 0)
-            else:
-                second_matmul(i - 1, 0)
-                store_half(i - 1, 0)
-                quantise_c(i - 1, 1)
-            second_matmul(i - 1, 1)
-            store_half(i - 1, 1)
+            for r in range(ROWS):
+                c_ps = psum.tile([P, PACK, P], F32, name="c_ps", tag="bank")
+                c_banks[(i, r)] = c_ps
+                for t in range(PACK):
+                    first_matmul(i, r, t)
+                weigh(i, r)
+                if r == 0:
+                    quantise_c(i - 1, HALF_ROWS)
+                    second_matmul(i - 1, 0)
+                    store_rows(i - 1, 0)
+                if r == 1 and not last:
+                    quantise_x(i + 1)
+                if r == 2 and not last:
+                    quantise_c(i, 0)
+                if last and r >= 1:
+                    quantise_c(i, r - 1, 1)
+                if r == (2 if last else ROWS - 1):
+                    second_matmul(i - 1, HALF_ROWS)
+                    store_rows(i - 1, HALF_ROWS)
             if i + LOOKAHEAD < N_CHUNKS:
                 for r in range(ROWS):
                     transpose_rows(i + LOOKAHEAD, r)
                     copy_rows(i + LOOKAHEAD, r, nc.scalar.copy)
+        quantise_c(N_CHUNKS - 1, ROWS - 1, 1)
+        for r in range(ROWS):
+            second_matmul(N_CHUNKS - 1, r, 1)
+            store_rows(N_CHUNKS - 1, r, 1, on_vector=(r == ROWS - 1))

@@ -304,18 +304,17 @@ def tile_gaussianlayer_t_kernel(tc, x, mus, log_vars, weights, out):
             gauss_in(t)
             transpose_gauss(t)
             transpose_rows(1, t)
-        square_out()
         quantise_x(0)
         copy_gauss(0, nc.vector.tensor_copy)
         copy_gauss(1, nc.vector.tensor_copy)
         quantise_gauss(0)
-        copy_gauss(2, nc.vector.tensor_copy)
+        copy_gauss(2, nc.scalar.copy)
         quantise_gauss(1)
         copy_gauss(3, nc.scalar.copy)
         quantise_gauss(2)
         quantise_gauss(3)
         for r in range(ROWS):
-            copy_rows(1, r, nc.scalar.copy if r < 2 else nc.vector.tensor_copy)
+            copy_rows(1, r, nc.scalar.copy)
         divisor = keep.tile([P, 1], F32, name="divisor")
         nc.vector.tensor_scalar(out=divisor[:], in0=w_sum[:], scalar1=float(IN), scalar2=None, op0=ALU.mult)
         inv_divisor = keep.tile([P, 1], F32, name="inv_divisor")
@@ -325,27 +324,23 @@ def tile_gaussianlayer_t_kernel(tc, x, mus, log_vars, weights, out):
         for r in range(ROWS):
             c_ps = psum.tile([P, PACK, P], F32, name="c_ps", tag="bank")
             c_banks[(0, r)] = c_ps
-        for step in range(PACK):
-            for t in range(step):
-                first_matmul(0, step, t)
-            for r in range(step + 1):
-                first_matmul(0, r, step)
+        for h in range(HALVES):
+            for t in range(PACK):
+                for s in range(HALF_ROWS):
+                    first_matmul(0, h * HALF_ROWS + s, t)
         planes = keep.tile([P, PACK, OUT], BF16, name="planes")
         gg_out = keep.tile([P, OUT, PACK], BF16, name="gg_out", align_bytes=64)
         gout_c = keep.tile([P, OUT], U32, name="gout_c", align_bytes=256)
         gout_s = keep.tile([P, OUT], U8, name="gout_s", align_bytes=256)
+        square_out()
         for t in range(PACK):
             nc.scalar.activation(
                 out=planes[:, t, :], in_=sq_out[t][:], func=ACT.Exp, bias=log_norm[1][:, t : t + 1],
                 scale=neg_steep[1][:, t : t + 1],
             )
-        quantise_x(1)
         weigh(0, 0)
-        nc.vector.tensor_copy(out=gg_out[:], in_=planes[:].rearrange("p t j -> p j t"))
         weigh(0, 1)
-        nc.vector.quantize_mx(
-            out=gout_c[:].bitcast(FP8X4), scales=gout_s[:], in_=gg_out[:].rearrange("p j t -> p (j t)")
-        )
+        quantise_x(1)
         weigh(0, 2)
         quantise_c(0, 0)
         weigh(0, 3)
@@ -353,6 +348,8 @@ def tile_gaussianlayer_t_kernel(tc, x, mus, log_vars, weights, out):
         for r in range(ROWS):
             transpose_rows(2, r)
             copy_rows(2, r, nc.scalar.copy)
+
+        pad = keep.tile([P, 800], F32, name="pad")
 
         for i in range(1, N_CHUNKS):
             last = i == N_CHUNKS - 1
@@ -366,10 +363,18 @@ def tile_gaussianlayer_t_kernel(tc, x, mus, log_vars, weights, out):
                 weigh(i, r)
                 if r == 0:
                     quantise_c(i - 1, HALF_ROWS)
+                    if i == 1:
+                        nc.vector.tensor_copy(out=gg_out[:], in_=planes[:].rearrange("p t j -> p j t"))
+                if r == 1 and i == 1:
+                    nc.vector.quantize_mx(
+                        out=gout_c[:].bitcast(FP8X4), scales=gout_s[:], in_=gg_out[:].rearrange("p j t -> p (j t)")
+                    )
+                if r == (2 if i == 1 else 0):
                     second_matmul(i - 1, 0)
                     store_rows(i - 1, 0)
                 if r == 1 and not last:
                     quantise_x(i + 1)
+                    nc.vector.memset(pad[:], 0.0)
                 if r == 2 and not last:
                     quantise_c(i, 0)
                 if last and r >= 1:

@@ -29,7 +29,8 @@ N_CHUNKS = BATCH // CHUNK
 X_BUFS = 8
 PRELOAD = 6
 MIDDLE = 0.5 * (IN - 1)
-VECTOR_FROM = 2
+VECTOR_FROM = 3
+AWAY = 1
 LOOKAHEAD = 2
 
 
@@ -71,8 +72,8 @@ def tile_gaussianlayer_t_kernel(tc, x, mus, log_vars, weights, out):
         nc.scalar.activation(out=warm_out[:], in_=warm[:], func=ACT.Exp)
         twos = keep.tile([P, PACK], F32, name="twos")
         nc.vector.memset(twos[:], 2.0)
-        ones_bf = keep.tile([P, P], BF16, name="ones_bf")
-        nc.vector.memset(ones_bf[:], 1.0)
+        spread_bf = keep.tile([P, P], BF16, name="spread_bf")
+        nc.vector.memset(spread_bf[:], float(IN))
         k_row = keep.tile([P, IN], F32, name="k_row")
         nc.gpsimd.iota(
             k_row[:, 0 : 2 * P], pattern=[[1, 2], [2, P]], base=0, channel_multiplier=0,
@@ -93,45 +94,36 @@ def tile_gaussianlayer_t_kernel(tc, x, mus, log_vars, weights, out):
         def by_axis(tile_ap, axis):
             return tile_ap.rearrange("p (t a) -> p t a", a=2)[:, :, axis]
 
-        spans = (IN - 1, OUT - 1)
-        neg_centre, neg_steep, log_norm = [], [], []
-        for axis, span in enumerate(spans):
-            centre = keep.tile([P, PACK], F32, name="centre%d" % axis)
-            nc.vector.tensor_scalar(
-                out=centre[:], in0=by_axis(mus_sb[:], axis), scalar1=-float(span), scalar2=None, op0=ALU.mult
+        def affine(engine, name, in_, factor, shift):
+            result = keep.tile([P, PACK], F32, name=name)
+            engine.tensor_scalar(
+                out=result[:], in0=in_, scalar1=factor, scalar2=shift, op0=ALU.mult, op1=ALU.add
             )
-            neg_centre.append(centre)
-        neg_twice = keep.tile([P, PACK], F32, name="neg_twice")
-        nc.vector.tensor_scalar(
-            out=neg_twice[:], in0=by_axis(mus_sb[:], 0), scalar1=-2.0 * (IN - 1), scalar2=2.0 * MIDDLE,
-            op0=ALU.mult, op1=ALU.add,
-        )
-        mid_centre = keep.tile([P, PACK], F32, name="mid_centre")
-        nc.vector.tensor_scalar(
-            out=mid_centre[:], in0=by_axis(mus_sb[:], 0), scalar1=-float(IN - 1), scalar2=MIDDLE,
-            op0=ALU.mult, op1=ALU.add,
-        )
+            return result
 
-        for axis, span in enumerate(spans):
-            power = keep.tile([P, PACK], F32, name="power%d" % axis)
-            nc.gpsimd.tensor_scalar(
-                out=power[:], in0=by_axis(lv_sb[:], axis), scalar1=-1.0 / math.log(2.0), scalar2=0.0,
-                op0=ALU.mult, op1=ALU.add,
-            )
+        spans = (IN - 1, OUT - 1)
+        neg_centre, neg_steep, log_norm = {}, {}, {}
+
+        def make_steep(axis):
+            log_var = by_axis(lv_sb[:], axis)
+            power = affine(nc.gpsimd, "power%d" % axis, log_var, -1.0 / math.log(2.0), 0.0)
             raised = keep.tile([P, PACK], F32, name="raised%d" % axis)
             nc.gpsimd.tensor_tensor(out=raised[:], in0=twos[:], in1=power[:], op=ALU.pow)
-            steep = keep.tile([P, PACK], F32, name="steep%d" % axis)
-            nc.gpsimd.tensor_scalar(
-                out=steep[:], in0=raised[:], scalar1=-0.5 / float(span * span), scalar2=0.0,
-                op0=ALU.mult, op1=ALU.add,
+            neg_steep[axis] = affine(
+                nc.gpsimd, "steep%d" % axis, raised[:], -0.5 / float(spans[axis] * spans[axis]), 0.0
             )
-            neg_steep.append(steep)
-            norm = keep.tile([P, PACK], F32, name="norm%d" % axis)
-            nc.vector.tensor_scalar(
-                out=norm[:], in0=by_axis(lv_sb[:], axis), scalar1=-0.5, scalar2=-0.5 * math.log(2.0 * math.pi),
-                op0=ALU.mult, op1=ALU.add,
+            log_norm[axis] = affine(
+                nc.gpsimd, "norm%d" % axis, log_var, -0.5, -0.5 * math.log(2.0 * math.pi)
             )
-            log_norm.append(norm)
+
+        def make_centre(engine, axis):
+            neg_centre[axis] = affine(
+                engine, "centre%d" % axis, by_axis(mus_sb[:], axis), -float(spans[axis]), 0.0
+            )
+
+        make_centre(nc.vector, 0)
+        neg_twice = affine(nc.vector, "neg_twice", by_axis(mus_sb[:], 0), -2.0 * (IN - 1), 2.0 * MIDDLE)
+        make_steep(0)
 
         sq_in, bias_in = {}, {}
         for t in range(PACK):
@@ -146,18 +138,19 @@ def tile_gaussianlayer_t_kernel(tc, x, mus, log_vars, weights, out):
                 out=sq_in[t][:], in0=mid_row[:], scalar=neg_twice[:, t : t + 1], in1=mid_row[:],
                 op0=ALU.add, op1=ALU.mult,
             )
+        mid_centre = affine(nc.gpsimd, "mid_centre", by_axis(mus_sb[:], 0), -float(IN - 1), MIDDLE)
+        lift = keep.tile([P, PACK], F32, name="lift")
+        nc.gpsimd.tensor_tensor(out=lift[:], in0=mid_centre[:], in1=mid_centre[:], op=ALU.mult)
+        lifted = keep.tile([P, PACK], F32, name="lifted")
+        nc.gpsimd.tensor_tensor(out=lifted[:], in0=lift[:], in1=neg_steep[0][:], op=ALU.mult)
+        biased = keep.tile([P, PACK], F32, name="biased")
+        nc.gpsimd.tensor_tensor(out=biased[:], in0=lifted[:], in1=log_norm[0][:], op=ALU.add)
+        for t in range(VECTOR_FROM, PACK):
+            bias_in[t] = biased[:, t : t + 1]
         w_f32 = keep.tile([P, PACK], F32, name="w_f32")
-        nc.vector.tensor_copy(out=w_f32[:], in_=w_sb[:])
-
-        def make_bias():
-            lift = keep.tile([P, PACK], F32, name="lift")
-            nc.vector.tensor_tensor(out=lift[:], in0=mid_centre[:], in1=mid_centre[:], op=ALU.mult)
-            lifted = keep.tile([P, PACK], F32, name="lifted")
-            nc.vector.tensor_tensor(out=lifted[:], in0=lift[:], in1=neg_steep[0][:], op=ALU.mult)
-            biased = keep.tile([P, PACK], F32, name="biased")
-            nc.vector.tensor_tensor(out=biased[:], in0=lifted[:], in1=log_norm[0][:], op=ALU.add)
-            for t in range(VECTOR_FROM, PACK):
-                bias_in[t] = biased[:, t : t + 1]
+        nc.gpsimd.tensor_copy(out=w_f32[:], in_=w_sb[:])
+        make_centre(nc.gpsimd, 1)
+        make_steep(1)
 
         sq_out = []
 
@@ -220,6 +213,18 @@ def tile_gaussianlayer_t_kernel(tc, x, mus, log_vars, weights, out):
             nc.vector.tensor_tensor(
                 out=gc_tiles[c][:, r * COMPS : (r + 1) * COMPS].rearrange("p (b t) -> p b t", t=PACK),
                 in0=c_banks[(c, r)][:].rearrange("p t b -> p b t"),
+                in1=w_f32[:].unsqueeze(1).to_broadcast([P, P, PACK]),
+                op=ALU.mult,
+            )
+
+        def weigh_away(c, r):
+            plain = stream.tile([P, COMPS], F32, name="plain")
+            nc.scalar.copy(
+                out=plain[:].rearrange("p (b t) -> p b t", t=PACK), in_=c_banks[(c, r)][:].rearrange("p t b -> p b t")
+            )
+            nc.gpsimd.tensor_tensor(
+                out=gc_tiles[c][:, r * COMPS : (r + 1) * COMPS].rearrange("p (b t) -> p b t", t=PACK),
+                in0=plain[:].rearrange("p (b t) -> p b t", t=PACK),
                 in1=w_f32[:].unsqueeze(1).to_broadcast([P, P, PACK]),
                 op=ALU.mult,
             )
@@ -291,10 +296,8 @@ def tile_gaussianlayer_t_kernel(tc, x, mus, log_vars, weights, out):
         for r in range(ROWS):
             transpose_rows(0, r)
             copy_rows(0, r, nc.vector.tensor_copy)
-            if r == 1:
-                make_bias()
         w_ps = psum.tile([P, HALF_ROWS * OUT], F32, name="w_ps", tag="bank")
-        nc.tensor.matmul(out=w_ps[:, 0:PACK], lhsT=ones_bf[:], rhs=w_sb[:], start=True, stop=True)
+        nc.tensor.matmul(out=w_ps[:, 0:PACK], lhsT=spread_bf[:], rhs=w_sb[:], start=True, stop=True)
         w_sum = keep.tile([P, 1], F32, name="w_sum")
         nc.vector.reduce_sum(out=w_sum[:], in_=w_ps[:, 0:PACK], axis=mybir.AxisListType.X)
         for t in range(PACK):
@@ -315,10 +318,8 @@ def tile_gaussianlayer_t_kernel(tc, x, mus, log_vars, weights, out):
         quantise_gauss(3)
         for r in range(ROWS):
             copy_rows(1, r, nc.scalar.copy)
-        divisor = keep.tile([P, 1], F32, name="divisor")
-        nc.vector.tensor_scalar(out=divisor[:], in0=w_sum[:], scalar1=float(IN), scalar2=None, op0=ALU.mult)
         inv_divisor = keep.tile([P, 1], F32, name="inv_divisor")
-        nc.vector.reciprocal(out=inv_divisor[:], in_=divisor[:])
+        nc.vector.reciprocal(out=inv_divisor[:], in_=w_sum[:])
 
 
         for r in range(ROWS):
@@ -349,39 +350,39 @@ def tile_gaussianlayer_t_kernel(tc, x, mus, log_vars, weights, out):
             transpose_rows(2, r)
             copy_rows(2, r, nc.scalar.copy)
 
-        pad = keep.tile([P, 800], F32, name="pad")
-
+        halves_done = 0
         for i in range(1, N_CHUNKS):
             last = i == N_CHUNKS - 1
             if i - 1 + PRELOAD < N_CHUNKS:
                 load_chunk(i - 1 + PRELOAD)
+            stands = () if i == 1 else (1, 2, 3) if i <= 3 else (1, 3)
+            if i >= 2:
+                quantise_c(i - 1, 0, ROWS)
             for r in range(ROWS):
                 c_ps = psum.tile([P, PACK, P], F32, name="c_ps", tag="bank")
                 c_banks[(i, r)] = c_ps
                 for t in range(PACK):
                     first_matmul(i, r, t)
-                weigh(i, r)
-                if r == 0:
-                    quantise_c(i - 1, HALF_ROWS)
-                    if i == 1:
-                        nc.vector.tensor_copy(out=gg_out[:], in_=planes[:].rearrange("p t j -> p j t"))
-                if r == 1 and i == 1:
+                if r != AWAY or last:
+                    weigh(i, r)
+                if i == 1 and r == 0:
+                    quantise_c(0, HALF_ROWS)
+                if i == 1 and r == 1:
+                    nc.vector.tensor_copy(out=gg_out[:], in_=planes[:].rearrange("p t j -> p j t"))
                     nc.vector.quantize_mx(
                         out=gout_c[:].bitcast(FP8X4), scales=gout_s[:], in_=gg_out[:].rearrange("p j t -> p (j t)")
                     )
-                if r == (2 if i == 1 else 0):
-                    second_matmul(i - 1, 0)
-                    store_rows(i - 1, 0)
+                if r in stands:
+                    chunk, half = divmod(halves_done, HALVES)
+                    second_matmul(chunk, half * HALF_ROWS)
+                    store_rows(chunk, half * HALF_ROWS)
+                    halves_done += 1
                 if r == 1 and not last:
                     quantise_x(i + 1)
-                    nc.vector.memset(pad[:], 0.0)
-                if r == 2 and not last:
-                    quantise_c(i, 0)
                 if last and r >= 1:
                     quantise_c(i, r - 1, 1)
-                if r == (2 if last else ROWS - 1):
-                    second_matmul(i - 1, HALF_ROWS)
-                    store_rows(i - 1, HALF_ROWS)
+                if r == AWAY and not last:
+                    weigh_away(i, r)
             if i + LOOKAHEAD < N_CHUNKS:
                 for r in range(ROWS):
                     transpose_rows(i + LOOKAHEAD, r)

@@ -28,9 +28,21 @@ CHUNK = ROWS * P
 N_CHUNKS = BATCH // CHUNK
 X_BUFS = 8
 PRELOAD = 6
-MIDDLE = 0.5 * (IN - 1)
-VECTOR_FROM = 3
+IN_BLOCKS = IN // (2 * P)
+OUT_BLOCKS = OUT // P
+N_BLOCKS = 2 * IN_BLOCKS + OUT_BLOCKS
+STEPS = (2 * P, P)
+PIECES = 3
+STRIDE = 4
+GROUPS = 2 + 2 * IN_BLOCKS
+LINEAR_ROW = 2 * STRIDE
+CONST_ROW = LINEAR_ROW + IN_BLOCKS * STRIDE
+NORM_ROW = 64
 AWAY = 1
+FIRST = "C M0 w0 M1 x S1 M2 w2 M3 w3 G0 G1 T0 T1 T2 T3 g"
+EARLY = "C M0 w0 M1 O x S1 M2 w2 M3 w3 O T0 T1 T2 T3"
+STEADY = "C M0 w0 M1 O x S1 M2 w2 M3 w3 O T0 T1 T2 T3"
+LAST = "C M0 w0 O M1 w1 O c0 M2 w2 O c1 M3 w3 O c2"
 LOOKAHEAD = 2
 
 
@@ -66,103 +78,120 @@ def tile_gaussianlayer_t_kernel(tc, x, mus, log_vars, weights, out):
         for c in range(1, PRELOAD):
             load_chunk(c)
 
-        warm = keep.tile([P, 1], F32, name="warm")
-        nc.vector.memset(warm[:], 0.0)
-        warm_out = keep.tile([P, 1], F32, name="warm_out")
-        nc.scalar.activation(out=warm_out[:], in_=warm[:], func=ACT.Exp)
-        twos = keep.tile([P, PACK], F32, name="twos")
+        twos = keep.tile([P, 2 * PACK], F32, name="twos")
         nc.vector.memset(twos[:], 2.0)
-        spread_bf = keep.tile([P, P], BF16, name="spread_bf")
-        nc.vector.memset(spread_bf[:], float(IN))
-        k_row = keep.tile([P, IN], F32, name="k_row")
+        warm_out = keep.tile([P, 1], F32, name="warm_out")
+        nc.scalar.activation(out=warm_out[:], in_=twos[:, 0:1], func=ACT.Exp)
+        offset = keep.tile([P, N_BLOCKS], F32, name="offset")
+        in_blocks = offset[:, 0 : 2 * IN_BLOCKS].rearrange("p (e b) -> p e b", e=2)
         nc.gpsimd.iota(
-            k_row[:, 0 : 2 * P], pattern=[[1, 2], [2, P]], base=0, channel_multiplier=0,
+            in_blocks, pattern=[[1, 2], [0, IN_BLOCKS]], base=-P, channel_multiplier=2,
             allow_small_or_imprecise_dtypes=True,
         )
-        for q in range(1, IN // (2 * P)):
-            nc.vector.tensor_scalar(
-                out=k_row[:, q * 2 * P : (q + 1) * 2 * P], in0=k_row[:, 0 : 2 * P],
-                scalar1=float(q * 2 * P), scalar2=None, op0=ALU.add,
-            )
+        nc.gpsimd.iota(
+            offset[:, 2 * IN_BLOCKS : N_BLOCKS], pattern=[[0, OUT_BLOCKS]], base=-P // 2, channel_multiplier=1,
+            allow_small_or_imprecise_dtypes=True,
+        )
+        ident_bf = keep.tile([P, P], BF16, name="ident_bf")
+        make_identity(nc, ident_bf[:])
         ident_f32 = keep.tile([P, P], F32, name="ident_f32")
         make_identity(nc, ident_f32[:])
-        ident_bf = keep.tile([P, P], BF16, name="ident_bf")
-        nc.vector.tensor_copy(out=ident_bf[:], in_=ident_f32[:])
-        mid_row = keep.tile([P, IN], F32, name="mid_row")
-        nc.vector.tensor_scalar(out=mid_row[:], in0=k_row[:], scalar1=-MIDDLE, scalar2=None, op0=ALU.add)
-
-        def by_axis(tile_ap, axis):
-            return tile_ap.rearrange("p (t a) -> p t a", a=2)[:, :, axis]
-
-        def affine(engine, name, in_, factor, shift):
-            result = keep.tile([P, PACK], F32, name=name)
-            engine.tensor_scalar(
-                out=result[:], in0=in_, scalar1=factor, scalar2=shift, op0=ALU.mult, op1=ALU.add
+        middle = keep.tile([P, 2, IN_BLOCKS], F32, name="middle")
+        for axis in range(2):
+            nc.gpsimd.iota(
+                middle[:, axis, :], pattern=[[STEPS[axis], IN_BLOCKS]], base=STEPS[axis] // 2, channel_multiplier=0,
+                allow_small_or_imprecise_dtypes=True,
             )
-            return result
+        basis_t = keep.tile([P, N_BLOCKS * P + P], BF16, name="basis_t")
+        nc.vector.memset(basis_t[:], 0.0)
+        coef_t = keep.tile([P, 2 * PACK, P], BF16, name="coef_t")
+        square = keep.tile([P, N_BLOCKS], F32, name="square")
+        nc.vector.tensor_tensor(out=square[:], in0=offset[:], in1=offset[:], op=ALU.mult)
+        by_block = basis_t[:, 0 : N_BLOCKS * P].rearrange("p (n k) -> p n k", k=P)
+        wide = [P, N_BLOCKS, PIECES]
+        nc.scalar.copy(out=by_block[:, :, 0:PIECES], in_=square[:].unsqueeze(2).to_broadcast(wide))
+        nc.vector.memset(coef_t[:], 0.0)
 
+        def staircase(first, count, row):
+            step = P + STRIDE
+            run = basis_t[:, first * P : first * P + count * step].rearrange("p (b k) -> p b k", k=step)
+            return run[:, :, row : row + PIECES]
+
+        groups = ((0, IN_BLOCKS), (IN_BLOCKS, IN_BLOCKS), (2 * IN_BLOCKS, OUT_BLOCKS))
+        for first, count in groups:
+            nc.scalar.copy(
+                out=staircase(first, count, LINEAR_ROW),
+                in_=offset[:, first : first + count].unsqueeze(2).to_broadcast([P, count, PIECES]),
+            )
+        for first, count in groups:
+            nc.vector.memset(staircase(first, count, CONST_ROW), 1.0)
+        nc.vector.memset(by_block[:, :, NORM_ROW : NORM_ROW + PIECES], 1.0)
+        nc.vector.tensor_tensor(
+            out=by_block[:, :, STRIDE : STRIDE + PIECES], in0=square[:].unsqueeze(2).to_broadcast(wide),
+            in1=by_block[:, :, 0:PIECES], op=ALU.subtract,
+        )
+        factors = keep.tile([P, 2, PACK, GROUPS], F32, name="factors")
         spans = (IN - 1, OUT - 1)
-        neg_centre, neg_steep, log_norm = {}, {}, {}
-
-        def make_steep(axis):
-            log_var = by_axis(lv_sb[:], axis)
-            power = affine(nc.gpsimd, "power%d" % axis, log_var, -1.0 / math.log(2.0), 0.0)
-            raised = keep.tile([P, PACK], F32, name="raised%d" % axis)
-            nc.gpsimd.tensor_tensor(out=raised[:], in0=twos[:], in1=power[:], op=ALU.pow)
-            neg_steep[axis] = affine(
-                nc.gpsimd, "steep%d" % axis, raised[:], -0.5 / float(spans[axis] * spans[axis]), 0.0
-            )
-            log_norm[axis] = affine(
-                nc.gpsimd, "norm%d" % axis, log_var, -0.5, -0.5 * math.log(2.0 * math.pi)
+        steep = [-0.5 / float(span * span) for span in spans]
+        for axis in range(2):
+            nc.vector.tensor_scalar(
+                out=factors[:, axis, :, 0:2], in0=twos[:].rearrange("p (t a) -> p t a", a=2),
+                scalar1=0.5 * steep[axis], scalar2=None, op0=ALU.mult,
             )
 
-        def make_centre(engine, axis):
-            neg_centre[axis] = affine(
-                engine, "centre%d" % axis, by_axis(mus_sb[:], axis), -float(spans[axis]), 0.0
-            )
-
-        make_centre(nc.vector, 0)
-        neg_twice = affine(nc.vector, "neg_twice", by_axis(mus_sb[:], 0), -2.0 * (IN - 1), 2.0 * MIDDLE)
-        make_steep(0)
-
-        sq_in, bias_in = {}, {}
-        for t in range(PACK):
-            sq_in[t] = keep.tile([P, IN], F32, name="sq%d" % t)
-            bias_in[t] = log_norm[0][:, t : t + 1]
-        for t in range(VECTOR_FROM):
-            nc.scalar.activation(
-                out=sq_in[t][:], in_=k_row[:], func=ACT.Square, bias=neg_centre[0][:, t : t + 1], scale=1.0
-            )
-        for t in range(VECTOR_FROM, PACK):
+        lv_by_axis = lv_sb[:].rearrange("p (t a) -> p a t", a=2)
+        mus_by_axis = mus_sb[:].rearrange("p (t a) -> p a t", a=2)
+        power = keep.tile([P, 2, PACK], F32, name="power")
+        nc.gpsimd.tensor_scalar(
+            out=power[:], in0=lv_by_axis, scalar1=-1.0 / math.log(2.0), scalar2=0.0, op0=ALU.mult, op1=ALU.add
+        )
+        raised = keep.tile([P, 2, PACK], F32, name="raised")
+        nc.gpsimd.tensor_tensor(
+            out=raised[:], in0=twos[:].rearrange("p (a t) -> p a t", a=2), in1=power[:], op=ALU.pow
+        )
+        distance = keep.tile([P, 2, PACK, IN_BLOCKS], F32, name="distance")
+        for axis in range(2):
             nc.vector.scalar_tensor_tensor(
-                out=sq_in[t][:], in0=mid_row[:], scalar=neg_twice[:, t : t + 1], in1=mid_row[:],
-                op0=ALU.add, op1=ALU.mult,
+                out=distance[:, axis], in0=mus_by_axis[:, axis, :].unsqueeze(2).to_broadcast([P, PACK, IN_BLOCKS]),
+                scalar=-float(spans[axis]), in1=middle[:, axis, :].unsqueeze(1).to_broadcast([P, PACK, IN_BLOCKS]),
+                op0=ALU.mult, op1=ALU.add,
             )
-        mid_centre = affine(nc.gpsimd, "mid_centre", by_axis(mus_sb[:], 0), -float(IN - 1), MIDDLE)
-        lift = keep.tile([P, PACK], F32, name="lift")
-        nc.gpsimd.tensor_tensor(out=lift[:], in0=mid_centre[:], in1=mid_centre[:], op=ALU.mult)
-        lifted = keep.tile([P, PACK], F32, name="lifted")
-        nc.gpsimd.tensor_tensor(out=lifted[:], in0=lift[:], in1=neg_steep[0][:], op=ALU.mult)
-        biased = keep.tile([P, PACK], F32, name="biased")
-        nc.gpsimd.tensor_tensor(out=biased[:], in0=lifted[:], in1=log_norm[0][:], op=ALU.add)
-        for t in range(VECTOR_FROM, PACK):
-            bias_in[t] = biased[:, t : t + 1]
+        norm = keep.tile([P, 2 * PACK, 1], F32, name="norm")
+        nc.vector.tensor_scalar(
+            out=norm[:].rearrange("p (a t) o -> p a (t o)", a=2), in0=lv_by_axis, scalar1=-0.5,
+            scalar2=-0.5 * math.log(2.0 * math.pi), op0=ALU.mult, op1=ALU.add,
+        )
+        all_rows = coef_t[:].rearrange("p q (g j) -> p q g j", j=STRIDE)
+        factors_flat = factors[:].rearrange("p a t g -> p (a t) g")
+        blocks = [P, 2 * PACK, IN_BLOCKS]
+        flat_distance = distance[:].rearrange("p a t b -> p (a t) b")
+        nc.vector.scalar_tensor_tensor(
+            out=factors_flat[:, :, 2 : 2 + IN_BLOCKS], in0=flat_distance, scalar=2.0,
+            in1=factors_flat[:, :, 0:1].to_broadcast(blocks), op0=ALU.mult, op1=ALU.mult,
+        )
+        nc.vector.tensor_copy(out=all_rows[:, :, NORM_ROW // STRIDE, 0:1], in_=norm[:])
+        nc.vector.scalar_tensor_tensor(
+            out=factors_flat[:, :, 2 + IN_BLOCKS : GROUPS], in0=factors_flat[:, :, 2 : 2 + IN_BLOCKS],
+            scalar=0.5, in1=flat_distance, op0=ALU.mult, op1=ALU.mult,
+        )
+
+        def split(value, first, count):
+            rows = all_rows[:, :, first : first + count, :]
+            rest = keep.tile([P, 2 * PACK, count], F32, name="rest%d" % first)
+            nc.vector.tensor_tensor(out=rest[:], in0=value, in1=rows[:, :, :, 0], op=ALU.subtract)
+            nc.vector.tensor_tensor(out=rows[:, :, :, 1], in0=value, in1=rows[:, :, :, 0], op=ALU.subtract)
+            nc.vector.tensor_tensor(out=rows[:, :, :, 2], in0=rest[:], in1=rows[:, :, :, 1], op=ALU.subtract)
+
+        split(norm[:], NORM_ROW // STRIDE, 1)
+        coef = keep.tile([P, 2 * PACK, GROUPS], F32, name="coef")
+        raised_wide = raised[:].rearrange("p a t -> p (a t)").unsqueeze(2).to_broadcast([P, 2 * PACK, GROUPS])
+        nc.vector.tensor_tensor(out=all_rows[:, :, 0:GROUPS, 0], in0=raised_wide, in1=factors_flat, op=ALU.mult)
+        nc.vector.tensor_tensor(out=coef[:], in0=raised_wide, in1=factors_flat, op=ALU.mult)
+        split(coef[:], 0, GROUPS)
         w_f32 = keep.tile([P, PACK], F32, name="w_f32")
         nc.gpsimd.tensor_copy(out=w_f32[:], in_=w_sb[:])
-        make_centre(nc.gpsimd, 1)
-        make_steep(1)
-
-        sq_out = []
-
-        def square_out():
-            for t in range(PACK):
-                sq_o = keep.tile([P, OUT], F32, name="sq_o%d" % t)
-                nc.scalar.activation(
-                    out=sq_o[:].rearrange("p (s e) -> p s e", e=2),
-                    in_=k_row[:, 0:OUT].rearrange("p (e s) -> p s e", e=2),
-                    func=ACT.Square, bias=neg_centre[1][:, t : t + 1], scale=1.0,
-                )
-                sq_out.append(sq_o)
+        spread_bf = keep.tile([P, P], BF16, name="spread_bf")
+        nc.gpsimd.memset(spread_bf[:], float(IN))
 
         xt_banks, gx_tiles, xc_tiles, xs_tiles = {}, {}, {}, {}
         gc_tiles, cc_tiles, cs_tiles = {}, {}, {}
@@ -205,11 +234,12 @@ def tile_gaussianlayer_t_kernel(tc, x, mus, log_vars, weights, out):
                     stop=(g == PASSES - 1),
                 )
 
+        def open_c(c):
+            gc_tiles[c] = stream.tile([P, ROWS * COMPS], BF16, name="gc", align_bytes=64)
+            cc_tiles[c] = stream.tile([P, ROWS * P], U32, name="cc", align_bytes=256)
+            cs_tiles[c] = stream.tile([P, ROWS * P], U8, name="cs", align_bytes=256)
+
         def weigh(c, r):
-            if r == 0:
-                gc_tiles[c] = stream.tile([P, ROWS * COMPS], BF16, name="gc", align_bytes=64)
-                cc_tiles[c] = stream.tile([P, ROWS * P], U32, name="cc", align_bytes=256)
-                cs_tiles[c] = stream.tile([P, ROWS * P], U8, name="cs", align_bytes=256)
             nc.vector.tensor_tensor(
                 out=gc_tiles[c][:, r * COMPS : (r + 1) * COMPS].rearrange("p (b t) -> p b t", t=PACK),
                 in0=c_banks[(c, r)][:].rearrange("p t b -> p b t"),
@@ -267,24 +297,31 @@ def tile_gaussianlayer_t_kernel(tc, x, mus, log_vars, weights, out):
         gg_in = keep.tile([P, PACK * PASSES * P * PACK], BF16, name="gg_in", align_bytes=64)
         gin_c = keep.tile([P, PACK * PASSES * P], U32, name="gin_c", align_bytes=256)
         gin_s = keep.tile([P, PACK * PASSES * P], U8, name="gin_s", align_bytes=256)
-        g_rows, g_banks = {}, {}
+        basis = keep.tile([P, N_BLOCKS, P], BF16, name="basis")
+        coef_rows = keep.tile([P, 2 * PACK, P], BF16, name="coef_rows")
+        e_banks = {}
 
-        def gauss_in(t):
-            g_t = stream.tile([P, IN], BF16, name="g_t", bufs=2)
+        def turn(out_tile, source, first, count, copy_out):
+            turned = psum.tile([P, PASSES * PACK, P], BF16, name="turned", tag="bank")
+            for n in range(count):
+                nc.tensor.transpose(turned[:, n, :], source[:, first + n, :], ident_bf[:])
+            copy_out(out=out_tile[:, first : first + count, :], in_=turned[:, 0:count, :])
+
+        def exponents_in(t, g):
+            e_ps = psum.tile([P, PACK, P], F32, name="e_ps", tag="bank")
+            for u in range(2):
+                for e in range(2):
+                    nc.tensor.matmul(
+                        out=e_ps[:, 2 * u + e, :], lhsT=basis[:, e * IN_BLOCKS + 2 * g + u, :], rhs=coef_rows[:, t, :],
+                        start=True, stop=True,
+                    )
+            e_banks[(t, g)] = e_ps
+
+        def gauss_in(t, g):
+            words = slice((t * PASSES + g) * COMPS, (t * PASSES + g + 1) * COMPS)
             nc.scalar.activation(
-                out=g_t[:], in_=sq_in[t][:], func=ACT.Exp, bias=bias_in[t], scale=neg_steep[0][:, t : t + 1]
-            )
-            g_rows[t] = g_t
-
-        def transpose_gauss(t):
-            g_ps = g_banks[t]
-            for j in range(PASSES * PACK):
-                nc.tensor.transpose(g_ps[:, j, :], g_rows[t][:, j * P : (j + 1) * P], ident_bf[:])
-
-        def copy_gauss(t, copy_out):
-            copy_out(
-                out=gg_in[:, t * IN : (t + 1) * IN].rearrange("p (g m k) -> p g m k", g=PASSES, k=PACK),
-                in_=g_banks[t][:].rearrange("p (g k) m -> p g m k", k=PACK),
+                out=gg_in[:, words].rearrange("p (m k) -> p m k", k=PACK),
+                in_=e_banks[(t, g)][:].rearrange("p k m -> p m k"), func=ACT.Exp,
             )
 
         def quantise_gauss(t):
@@ -293,59 +330,68 @@ def tile_gaussianlayer_t_kernel(tc, x, mus, log_vars, weights, out):
                 out=gin_c[:, words].bitcast(FP8X4), scales=gin_s[:, words], in_=gg_in[:, t * IN : (t + 1) * IN]
             )
 
-        for r in range(ROWS):
-            transpose_rows(0, r)
-            copy_rows(0, r, nc.vector.tensor_copy)
-        w_ps = psum.tile([P, HALF_ROWS * OUT], F32, name="w_ps", tag="bank")
-        nc.tensor.matmul(out=w_ps[:, 0:PACK], lhsT=spread_bf[:], rhs=w_sb[:], start=True, stop=True)
-        w_sum = keep.tile([P, 1], F32, name="w_sum")
-        nc.vector.reduce_sum(out=w_sum[:], in_=w_ps[:, 0:PACK], axis=mybir.AxisListType.X)
-        for t in range(PACK):
-            g_ps = psum.tile([P, PASSES * PACK, P], BF16, name="g_ps", tag="bank")
-            g_banks[t] = g_ps
-        for t in range(PACK):
-            gauss_in(t)
-            transpose_gauss(t)
-            transpose_rows(1, t)
-        quantise_x(0)
-        copy_gauss(0, nc.vector.tensor_copy)
-        copy_gauss(1, nc.vector.tensor_copy)
-        quantise_gauss(0)
-        copy_gauss(2, nc.scalar.copy)
-        quantise_gauss(1)
-        copy_gauss(3, nc.scalar.copy)
-        quantise_gauss(2)
-        quantise_gauss(3)
-        for r in range(ROWS):
-            copy_rows(1, r, nc.scalar.copy)
-        inv_divisor = keep.tile([P, 1], F32, name="inv_divisor")
-        nc.vector.reciprocal(out=inv_divisor[:], in_=w_sum[:])
-
-
-        for r in range(ROWS):
-            c_ps = psum.tile([P, PACK, P], F32, name="c_ps", tag="bank")
-            c_banks[(0, r)] = c_ps
-        for h in range(HALVES):
+        def gauss_out(h):
+            e_ps = psum.tile([P, PACK, P], F32, name="e_ps", tag="bank")
             for t in range(PACK):
-                for s in range(HALF_ROWS):
-                    first_matmul(0, h * HALF_ROWS + s, t)
-        planes = keep.tile([P, PACK, OUT], BF16, name="planes")
+                nc.tensor.matmul(
+                    out=e_ps[:, t, :], lhsT=coef_rows[:, PACK + t, :], rhs=basis[:, 2 * IN_BLOCKS + h, :],
+                    start=True, stop=True,
+                )
+            nc.scalar.activation(
+                out=gg_out[:, h * P : (h + 1) * P, :], in_=e_ps[:].rearrange("p t j -> p j t"), func=ACT.Exp
+            )
+
         gg_out = keep.tile([P, OUT, PACK], BF16, name="gg_out", align_bytes=64)
         gout_c = keep.tile([P, OUT], U32, name="gout_c", align_bytes=256)
         gout_s = keep.tile([P, OUT], U8, name="gout_s", align_bytes=256)
-        square_out()
-        for t in range(PACK):
-            nc.scalar.activation(
-                out=planes[:, t, :], in_=sq_out[t][:], func=ACT.Exp, bias=log_norm[1][:, t : t + 1],
-                scale=neg_steep[1][:, t : t + 1],
-            )
-        weigh(0, 0)
-        weigh(0, 1)
-        quantise_x(1)
-        weigh(0, 2)
-        quantise_c(0, 0)
-        weigh(0, 3)
 
+        turn(basis, by_block, 0, 2 * IN_BLOCKS, nc.scalar.copy)
+        turn(basis, by_block, 2 * IN_BLOCKS, OUT_BLOCKS, nc.scalar.copy)
+        for r in range(ROWS):
+            transpose_rows(0, r)
+            copy_rows(0, r, nc.scalar.copy if r < 2 else nc.vector.tensor_copy)
+        turned = psum.tile([P, 2 * PACK, P], BF16, name="turned", tag="bank")
+        for q in range(2 * PACK):
+            nc.tensor.transpose(turned[:, q, :], coef_t[:, q, :], ident_bf[:])
+        nc.scalar.copy(out=coef_rows[:, 0:PACK, :], in_=turned[:, 0:PACK, :])
+        quantise_x(0)
+        nc.vector.tensor_copy(out=coef_rows[:, PACK : 2 * PACK, :], in_=turned[:, PACK : 2 * PACK, :])
+        for t in range(PACK // 2):
+            for g in range(PASSES):
+                exponents_in(t, g)
+                gauss_in(t, g)
+        for r in range(ROWS):
+            transpose_rows(1, r)
+        quantise_gauss(0)
+        for r in range(HALF_ROWS):
+            copy_rows(1, r, nc.vector.tensor_copy)
+        quantise_gauss(1)
+        for r in range(HALF_ROWS, ROWS):
+            copy_rows(1, r, nc.vector.tensor_copy)
+        w_ps = psum.tile([P, HALF_ROWS * OUT], F32, name="w_ps", tag="bank")
+        nc.tensor.matmul(out=w_ps[:, 0:PACK], lhsT=spread_bf[:], rhs=w_sb[:], start=True, stop=True)
+        w_sum = keep.tile([P, 1], F32, name="w_sum")
+        inv_divisor = keep.tile([P, 1], F32, name="inv_divisor")
+        nc.vector.reduce_sum(out=w_sum[:], in_=w_ps[:, 0:PACK], axis=mybir.AxisListType.X)
+        for t in range(PACK // 2, PACK):
+            for g in range(PASSES):
+                exponents_in(t, g)
+                gauss_in(t, g)
+        quantise_gauss(2)
+        quantise_gauss(3)
+        quantise_x(1)
+        for r in range(ROWS):
+            c_ps = psum.tile([P, PACK, P], F32, name="c_ps", tag="bank")
+            c_banks[(0, r)] = c_ps
+        for t in range(PACK):
+            for r in range(ROWS):
+                first_matmul(0, r, t)
+        open_c(0)
+        weigh(0, 0)
+        nc.vector.reciprocal(out=inv_divisor[:], in_=w_sum[:])
+        weigh_away(0, 1)
+        weigh(0, 2)
+        weigh(0, 3)
         for r in range(ROWS):
             transpose_rows(2, r)
             copy_rows(2, r, nc.scalar.copy)
@@ -353,40 +399,48 @@ def tile_gaussianlayer_t_kernel(tc, x, mus, log_vars, weights, out):
         halves_done = 0
         for i in range(1, N_CHUNKS):
             last = i == N_CHUNKS - 1
+            open_c(i)
             if i - 1 + PRELOAD < N_CHUNKS:
                 load_chunk(i - 1 + PRELOAD)
-            stands = () if i == 1 else (1, 2, 3) if i <= 3 else (1, 3)
-            if i >= 2:
-                quantise_c(i - 1, 0, ROWS)
-            for r in range(ROWS):
-                c_ps = psum.tile([P, PACK, P], F32, name="c_ps", tag="bank")
-                c_banks[(i, r)] = c_ps
-                for t in range(PACK):
-                    first_matmul(i, r, t)
-                if r != AWAY or last:
+            steps = FIRST if i == 1 else EARLY if i <= 3 else LAST if last else STEADY
+            for token in steps.split():
+                kind, r = token[0], int(token[1:] or 0)
+                if kind == "M":
+                    c_ps = psum.tile([P, PACK, P], F32, name="c_ps", tag="bank")
+                    c_banks[(i, r)] = c_ps
+                    for t in range(PACK):
+                        first_matmul(i, r, t)
+                elif kind == "w":
                     weigh(i, r)
-                if i == 1 and r == 0:
+                elif kind == "S":
+                    weigh_away(i, r)
+                elif kind == "C":
+                    quantise_c(i - 1, 0, ROWS)
+                elif kind == "c":
+                    quantise_c(i, r, 1)
+                elif kind == "h":
                     quantise_c(0, HALF_ROWS)
-                if i == 1 and r == 1:
-                    nc.vector.tensor_copy(out=gg_out[:], in_=planes[:].rearrange("p t j -> p j t"))
+                elif kind == "x":
+                    quantise_x(i + 1)
+                elif kind == "g":
                     nc.vector.quantize_mx(
                         out=gout_c[:].bitcast(FP8X4), scales=gout_s[:], in_=gg_out[:].rearrange("p j t -> p (j t)")
                     )
-                if r in stands:
+                elif kind == "G":
+                    gauss_out(r)
+                elif kind == "O":
                     chunk, half = divmod(halves_done, HALVES)
                     second_matmul(chunk, half * HALF_ROWS)
                     store_rows(chunk, half * HALF_ROWS)
                     halves_done += 1
-                if r == 1 and not last:
-                    quantise_x(i + 1)
-                if last and r >= 1:
-                    quantise_c(i, r - 1, 1)
-                if r == AWAY and not last:
-                    weigh_away(i, r)
-            if i + LOOKAHEAD < N_CHUNKS:
-                for r in range(ROWS):
+                elif kind == "T" and i + LOOKAHEAD < N_CHUNKS:
                     transpose_rows(i + LOOKAHEAD, r)
                     copy_rows(i + LOOKAHEAD, r, nc.scalar.copy)
+        while halves_done < HALVES * (N_CHUNKS - 1):
+            chunk, half = divmod(halves_done, HALVES)
+            second_matmul(chunk, half * HALF_ROWS)
+            store_rows(chunk, half * HALF_ROWS)
+            halves_done += 1
         quantise_c(N_CHUNKS - 1, ROWS - 1, 1)
         for r in range(ROWS):
             second_matmul(N_CHUNKS - 1, r, 1)

@@ -18,6 +18,12 @@ FLOPS = 2 * BATCH * IN * COMPS + 2 * BATCH * COMPS * OUT
 P = 128
 PACK = 4
 K_PASS = P * PACK
+TURNED = (9,)
+BLOCK = 32
+PRE = {5: [(9, 0, 8)], 6: [(9, 8, 8)]}
+STEPLOAD = {}
+UP = 3
+TURN_TOKEN = "w3"
 BANKS = 8
 HALF_IN = IN // 2
 PASSES = IN // K_PASS
@@ -27,7 +33,7 @@ HALF_ROWS = ROWS // HALVES
 CHUNK = ROWS * P
 N_CHUNKS = BATCH // CHUNK
 X_BUFS = 8
-PRELOAD = 6
+PRELOAD = 7
 IN_BLOCKS = IN // (2 * P)
 OUT_BLOCKS = OUT // P
 N_BLOCKS = 2 * IN_BLOCKS + OUT_BLOCKS
@@ -39,9 +45,11 @@ LINEAR_ROW = 2 * STRIDE
 CONST_ROW = LINEAR_ROW + IN_BLOCKS * STRIDE
 NORM_ROW = 64
 AWAY = 1
-FIRST = "C M0 w0 M1 x S1 M2 w2 M3 w3 G0 G1 T0 T1 T2 T3 g"
+FIRST = "M0 w0 C M1 x S1 M2 w2 M3 w3 G0 G1 T0 T1 T2 T3 g"
 EARLY = "C M0 w0 M1 O x S1 M2 w2 M3 w3 O T0 T1 T2 T3"
 STEADY = "C M0 w0 M1 O x S1 M2 w2 M3 w3 O T0 T1 T2 T3"
+ENDQ = (3,)
+NEXT = "C M0 w0 M1 O x S1 M2 w2 M3 w3 O T0 T1 T2 T3"
 LAST = "C M0 w0 O M1 w1 O c0 M2 w2 O c1 M3 w3 O c2"
 LOOKAHEAD = 2
 
@@ -52,6 +60,8 @@ def tile_gaussianlayer_t_kernel(tc, x, mus, log_vars, weights, out):
         keep = ctx.enter_context(tc.tile_pool(name="keep", bufs=1))
         x_pool = ctx.enter_context(tc.tile_pool(name="x_pool", bufs=X_BUFS))
         stream = ctx.enter_context(tc.tile_pool(name="stream", bufs=3))
+        turned_pool = ctx.enter_context(tc.tile_pool(name="turned_pool", bufs=1))
+        tx_pool = ctx.enter_context(tc.tile_pool(name="tx_pool", bufs=1))
         psum = ctx.enter_context(tc.psum_pool(name="psum", bufs=BANKS))
         ctx.enter_context(tc.manual_schedule())
 
@@ -65,7 +75,26 @@ def tile_gaussianlayer_t_kernel(tc, x, mus, log_vars, weights, out):
 
         x_tiles = {}
 
+        turned_x = {}
+
+        def load_turned(c, first_piece, count):
+            if first_piece == 0:
+                turned_x[c] = tx_pool.tile([P, ROWS * IN], BF16, name="turned_x", align_bytes=64)
+            rows = x[c * CHUNK : (c + 1) * CHUNK, :].rearrange("(j b) k -> b j k", b=BLOCK // 2)
+            for piece in range(first_piece, first_piece + count):
+                g, u, q = piece // 8, piece // 4 % 2, piece % 4
+                first = g * K_PASS + u * 2 * P + q * 2 * BLOCK
+                width = ROWS * IN // PASSES
+                nc.sync.dma_start(
+                    out=turned_x[c][q * BLOCK + u : (q + 1) * BLOCK : 2, g * width : (g + 1) * width].rearrange(
+                        "p (j w) -> p j w", w=2 * BLOCK
+                    ),
+                    in_=rows[:, :, first : first + 2 * BLOCK],
+                )
+
         def load_chunk(c, pieces=1):
+            if c in TURNED:
+                return
             x_sb = x_pool.tile([P, ROWS * IN], BF16, name="x_sb")
             rows = x[c * CHUNK : (c + 1) * CHUNK, :].rearrange("(p r) k -> p (r k)", r=ROWS)
             width = ROWS * IN // pieces
@@ -77,6 +106,8 @@ def tile_gaussianlayer_t_kernel(tc, x, mus, log_vars, weights, out):
         load_chunk(0, pieces=2)
         for c in range(1, PRELOAD):
             load_chunk(c)
+            for a, b, n in PRE.get(c, ()):
+                load_turned(a, b, n)
 
         twos = keep.tile([P, 2 * PACK], F32, name="twos")
         nc.vector.memset(twos[:], 2.0)
@@ -103,14 +134,14 @@ def tile_gaussianlayer_t_kernel(tc, x, mus, log_vars, weights, out):
                 allow_small_or_imprecise_dtypes=True,
             )
         basis_t = keep.tile([P, N_BLOCKS * P + P], BF16, name="basis_t")
-        nc.vector.memset(basis_t[:], 0.0)
+        nc.vector.memset(basis_t[:].bitcast(F32), 0.0)
         coef_t = keep.tile([P, 2 * PACK, P], BF16, name="coef_t")
         square = keep.tile([P, N_BLOCKS], F32, name="square")
         nc.vector.tensor_tensor(out=square[:], in0=offset[:], in1=offset[:], op=ALU.mult)
         by_block = basis_t[:, 0 : N_BLOCKS * P].rearrange("p (n k) -> p n k", k=P)
         wide = [P, N_BLOCKS, PIECES]
         nc.scalar.copy(out=by_block[:, :, 0:PIECES], in_=square[:].unsqueeze(2).to_broadcast(wide))
-        nc.vector.memset(coef_t[:], 0.0)
+        nc.vector.memset(coef_t[:].rearrange("p q k -> p (q k)").bitcast(F32), 0.0)
 
         def staircase(first, count, row):
             step = P + STRIDE
@@ -130,6 +161,8 @@ def tile_gaussianlayer_t_kernel(tc, x, mus, log_vars, weights, out):
             out=by_block[:, :, STRIDE : STRIDE + PIECES], in0=square[:].unsqueeze(2).to_broadcast(wide),
             in1=by_block[:, :, 0:PIECES], op=ALU.subtract,
         )
+        spread_bf = keep.tile([P, P], BF16, name="spread_bf")
+        nc.vector.memset(spread_bf[:], float(IN))
         factors = keep.tile([P, 2, PACK, GROUPS], F32, name="factors")
         spans = (IN - 1, OUT - 1)
         steep = [-0.5 / float(span * span) for span in spans]
@@ -182,16 +215,8 @@ def tile_gaussianlayer_t_kernel(tc, x, mus, log_vars, weights, out):
             nc.vector.tensor_tensor(out=rows[:, :, :, 1], in0=value, in1=rows[:, :, :, 0], op=ALU.subtract)
             nc.vector.tensor_tensor(out=rows[:, :, :, 2], in0=rest[:], in1=rows[:, :, :, 1], op=ALU.subtract)
 
-        split(norm[:], NORM_ROW // STRIDE, 1)
-        coef = keep.tile([P, 2 * PACK, GROUPS], F32, name="coef")
-        raised_wide = raised[:].rearrange("p a t -> p (a t)").unsqueeze(2).to_broadcast([P, 2 * PACK, GROUPS])
-        nc.vector.tensor_tensor(out=all_rows[:, :, 0:GROUPS, 0], in0=raised_wide, in1=factors_flat, op=ALU.mult)
-        nc.vector.tensor_tensor(out=coef[:], in0=raised_wide, in1=factors_flat, op=ALU.mult)
-        split(coef[:], 0, GROUPS)
         w_f32 = keep.tile([P, PACK], F32, name="w_f32")
         nc.gpsimd.tensor_copy(out=w_f32[:], in_=w_sb[:])
-        spread_bf = keep.tile([P, P], BF16, name="spread_bf")
-        nc.gpsimd.memset(spread_bf[:], float(IN))
 
         xt_banks, gx_tiles, xc_tiles, xs_tiles = {}, {}, {}, {}
         gc_tiles, cc_tiles, cs_tiles = {}, {}, {}
@@ -214,6 +239,12 @@ def tile_gaussianlayer_t_kernel(tc, x, mus, log_vars, weights, out):
                 in_=xt_banks[(c, r)][:].rearrange("p (g u) b -> p g b u", u=2),
             )
 
+        def turn_rows(c, r):
+            if r == 0:
+                gx_tiles[c] = turned_pool.tile([P, ROWS * IN], BF16, name="gx_turned", align_bytes=64)
+            words = slice(r * HALF_IN, (r + 1) * HALF_IN)
+            nc.vector.transpose(out=gx_tiles[c][:].bitcast(F32)[:, words], in_=turned_x[c][:].bitcast(F32)[:, words])
+
         def quantise_x(c):
             xc = stream.tile([P, ROWS * PASSES * P], U32, name="xc", align_bytes=256, bufs=LOOKAHEAD + 2)
             xs = stream.tile([P, ROWS * PASSES * P], U8, name="xs", align_bytes=256, bufs=LOOKAHEAD + 2)
@@ -223,7 +254,8 @@ def tile_gaussianlayer_t_kernel(tc, x, mus, log_vars, weights, out):
         def first_matmul(c, r, t):
             for g in range(PASSES):
                 w_cols = slice((t * PASSES + g) * P, (t * PASSES + g + 1) * P)
-                x_cols = slice((r * PASSES + g) * P, (r * PASSES + g + 1) * P)
+                first = g * ROWS + r if c in TURNED else r * PASSES + g
+                x_cols = slice(first * P, (first + 1) * P)
                 nc.tensor.matmul_mx(
                     out=c_banks[(c, r)][:, t, :],
                     lhsT=gin_c[:, w_cols].bitcast(FP8X4),
@@ -291,8 +323,14 @@ def tile_gaussianlayer_t_kernel(tc, x, mus, log_vars, weights, out):
                 )
             else:
                 nc.scalar.activation(out=o_sb[:, cols], in_=bank, func=ACT.Copy, scale=inv_divisor[:, 0:1])
-            chunk = out[c * CHUNK : (c + 1) * CHUNK, :].rearrange("(p r) j -> p (r j)", r=ROWS)
-            nc.sync.dma_start(out=chunk[:, first * OUT : (first + rows) * OUT], in_=o_sb[:, cols])
+            chunk = out[c * CHUNK : (c + 1) * CHUNK, :]
+            if c in TURNED:
+                chunk = chunk.rearrange("(r p) j -> p r j", p=P)
+            else:
+                chunk = chunk.rearrange("(p r) j -> p r j", r=ROWS)
+            nc.sync.dma_start(
+                out=chunk[:, first : first + rows, :], in_=o_sb[:, cols].rearrange("p (r j) -> p r j", j=OUT)
+            )
 
         gg_in = keep.tile([P, PACK * PASSES * P * PACK], BF16, name="gg_in", align_bytes=64)
         gin_c = keep.tile([P, PACK * PASSES * P], U32, name="gin_c", align_bytes=256)
@@ -347,6 +385,17 @@ def tile_gaussianlayer_t_kernel(tc, x, mus, log_vars, weights, out):
 
         turn(basis, by_block, 0, 2 * IN_BLOCKS, nc.scalar.copy)
         turn(basis, by_block, 2 * IN_BLOCKS, OUT_BLOCKS, nc.scalar.copy)
+        w_ps = psum.tile([P, HALF_ROWS * OUT], F32, name="w_ps", tag="bank")
+        nc.tensor.matmul(out=w_ps[:, 0:PACK], lhsT=spread_bf[:], rhs=w_sb[:], start=True, stop=True)
+        w_sum = keep.tile([P, 1], F32, name="w_sum")
+        inv_divisor = keep.tile([P, 1], F32, name="inv_divisor")
+        split(norm[:], NORM_ROW // STRIDE, 1)
+        nc.vector.reduce_sum(out=w_sum[:], in_=w_ps[:, 0:PACK], axis=mybir.AxisListType.X)
+        coef = keep.tile([P, 2 * PACK, GROUPS], F32, name="coef")
+        raised_wide = raised[:].rearrange("p a t -> p (a t)").unsqueeze(2).to_broadcast([P, 2 * PACK, GROUPS])
+        nc.vector.tensor_tensor(out=all_rows[:, :, 0:GROUPS, 0], in0=raised_wide, in1=factors_flat, op=ALU.mult)
+        nc.vector.tensor_tensor(out=coef[:], in0=raised_wide, in1=factors_flat, op=ALU.mult)
+        split(coef[:], 0, GROUPS)
         for r in range(ROWS):
             transpose_rows(0, r)
             copy_rows(0, r, nc.scalar.copy if r < 2 else nc.vector.tensor_copy)
@@ -362,17 +411,12 @@ def tile_gaussianlayer_t_kernel(tc, x, mus, log_vars, weights, out):
                 gauss_in(t, g)
         for r in range(ROWS):
             transpose_rows(1, r)
+        copy_rows(1, 0, nc.vector.tensor_copy)
         quantise_gauss(0)
-        for r in range(HALF_ROWS):
-            copy_rows(1, r, nc.vector.tensor_copy)
+        copy_rows(1, 1, nc.vector.tensor_copy)
         quantise_gauss(1)
         for r in range(HALF_ROWS, ROWS):
             copy_rows(1, r, nc.vector.tensor_copy)
-        w_ps = psum.tile([P, HALF_ROWS * OUT], F32, name="w_ps", tag="bank")
-        nc.tensor.matmul(out=w_ps[:, 0:PACK], lhsT=spread_bf[:], rhs=w_sb[:], start=True, stop=True)
-        w_sum = keep.tile([P, 1], F32, name="w_sum")
-        inv_divisor = keep.tile([P, 1], F32, name="inv_divisor")
-        nc.vector.reduce_sum(out=w_sum[:], in_=w_ps[:, 0:PACK], axis=mybir.AxisListType.X)
         for t in range(PACK // 2, PACK):
             for g in range(PASSES):
                 exponents_in(t, g)
@@ -383,26 +427,44 @@ def tile_gaussianlayer_t_kernel(tc, x, mus, log_vars, weights, out):
         for r in range(ROWS):
             c_ps = psum.tile([P, PACK, P], F32, name="c_ps", tag="bank")
             c_banks[(0, r)] = c_ps
-        for t in range(PACK):
-            for r in range(ROWS):
+        for t in range(PACK // 2):
+            for r in range(HALF_ROWS):
                 first_matmul(0, r, t)
+        for r in range(HALF_ROWS):
+            transpose_rows(2, r)
+        for t in range(PACK // 2):
+            for r in range(HALF_ROWS, ROWS):
+                first_matmul(0, r, t)
+        for r in range(ROWS):
+            first_matmul(0, r, 2)
+        for r in range(ROWS):
+            first_matmul(0, r, 3)
+        for r in range(HALF_ROWS, ROWS):
+            transpose_rows(2, r)
+        for r in range(HALF_ROWS):
+            copy_rows(2, r, nc.scalar.copy)
         open_c(0)
         weigh(0, 0)
         nc.vector.reciprocal(out=inv_divisor[:], in_=w_sum[:])
         weigh_away(0, 1)
         weigh(0, 2)
         weigh(0, 3)
-        for r in range(ROWS):
-            transpose_rows(2, r)
+        for r in range(HALF_ROWS, ROWS):
             copy_rows(2, r, nc.scalar.copy)
 
         halves_done = 0
+        upright = [(c, r) for c in range(LOOKAHEAD + 1, N_CHUNKS) if c not in TURNED for r in range(ROWS)]
+        rows_done = 0
+        turn_list = [(c, r) for c in TURNED for r in range(ROWS)]
+        turns_done = 0
         for i in range(1, N_CHUNKS):
             last = i == N_CHUNKS - 1
             open_c(i)
             if i - 1 + PRELOAD < N_CHUNKS:
                 load_chunk(i - 1 + PRELOAD)
-            steps = FIRST if i == 1 else EARLY if i <= 3 else LAST if last else STEADY
+            for a, b, n in STEPLOAD.get(i, ()):
+                load_turned(a, b, n)
+            steps = FIRST if i == 1 else EARLY if i <= 3 else LAST if last else NEXT if i == N_CHUNKS - 2 else STEADY
             for token in steps.split():
                 kind, r = token[0], int(token[1:] or 0)
                 if kind == "M":
@@ -433,15 +495,24 @@ def tile_gaussianlayer_t_kernel(tc, x, mus, log_vars, weights, out):
                     second_matmul(chunk, half * HALF_ROWS)
                     store_rows(chunk, half * HALF_ROWS)
                     halves_done += 1
-                elif kind == "T" and i + LOOKAHEAD < N_CHUNKS:
-                    transpose_rows(i + LOOKAHEAD, r)
-                    copy_rows(i + LOOKAHEAD, r, nc.scalar.copy)
+                elif kind == "T" and r == 0:
+                    needed = len([c for c, rr in upright if c <= i + LOOKAHEAD])
+                    due = max(needed, min(rows_done + UP, len(upright)))
+                    while rows_done < due:
+                        c, rr = upright[rows_done]
+                        transpose_rows(c, rr)
+                        copy_rows(c, rr, nc.scalar.copy)
+                        rows_done += 1
+                for a in TURNED:
+                    if token == TURN_TOKEN and 0 <= i - a + 5 < ROWS:
+                        turn_rows(a, i - a + 5)
         while halves_done < HALVES * (N_CHUNKS - 1):
             chunk, half = divmod(halves_done, HALVES)
             second_matmul(chunk, half * HALF_ROWS)
             store_rows(chunk, half * HALF_ROWS)
             halves_done += 1
-        quantise_c(N_CHUNKS - 1, ROWS - 1, 1)
+        for r in ENDQ:
+            quantise_c(N_CHUNKS - 1, r, 1)
         for r in range(ROWS):
             second_matmul(N_CHUNKS - 1, r, 1)
             store_rows(N_CHUNKS - 1, r, 1, on_vector=(r == ROWS - 1))

@@ -18,10 +18,10 @@ FLOPS = 2 * BATCH * IN * COMPS + 2 * BATCH * COMPS * OUT
 P = 128
 PACK = 4
 K_PASS = P * PACK
-TURNED = (9,)
+TURNED = (8, 14)
 BLOCK = 32
-PRE = {5: [(9, 0, 8)], 6: [(9, 8, 8)]}
-STEPLOAD = {}
+PRE = {5: [(8, 0, 8)], 6: [(8, 8, 8)]}
+STEPLOAD = {5: [(14, 0, 4)], 6: [(14, 4, 4)], 7: [(14, 8, 4)], 8: [(14, 12, 4)]}
 UP = 3
 TURN_TOKEN = "w3"
 BANKS = 8
@@ -61,7 +61,7 @@ def tile_gaussianlayer_t_kernel(tc, x, mus, log_vars, weights, out):
         x_pool = ctx.enter_context(tc.tile_pool(name="x_pool", bufs=X_BUFS))
         stream = ctx.enter_context(tc.tile_pool(name="stream", bufs=3))
         turned_pool = ctx.enter_context(tc.tile_pool(name="turned_pool", bufs=1))
-        tx_pool = ctx.enter_context(tc.tile_pool(name="tx_pool", bufs=1))
+        tx_pool = ctx.enter_context(tc.tile_pool(name="tx_pool", bufs=2))
         psum = ctx.enter_context(tc.psum_pool(name="psum", bufs=BANKS))
         ctx.enter_context(tc.manual_schedule())
 
@@ -291,6 +291,13 @@ def tile_gaussianlayer_t_kernel(tc, x, mus, log_vars, weights, out):
                 op=ALU.mult,
             )
 
+        def weigh_scalar(c, r):
+            values = gc_tiles[c][:, r * COMPS : (r + 1) * COMPS].rearrange("p (b t) -> p b t", t=PACK)
+            for t in range(PACK):
+                nc.scalar.activation(
+                    out=values[:, :, t], in_=c_banks[(c, r)][:, t, :], func=ACT.Copy, scale=w_f32[:, t : t + 1]
+                )
+
         def quantise_c(c, first, rows=HALF_ROWS):
             words = slice(first * P, (first + rows) * P)
             values = slice(first * COMPS, (first + rows) * COMPS)
@@ -390,7 +397,6 @@ def tile_gaussianlayer_t_kernel(tc, x, mus, log_vars, weights, out):
         w_sum = keep.tile([P, 1], F32, name="w_sum")
         inv_divisor = keep.tile([P, 1], F32, name="inv_divisor")
         split(norm[:], NORM_ROW // STRIDE, 1)
-        nc.vector.reduce_sum(out=w_sum[:], in_=w_ps[:, 0:PACK], axis=mybir.AxisListType.X)
         coef = keep.tile([P, 2 * PACK, GROUPS], F32, name="coef")
         raised_wide = raised[:].rearrange("p a t -> p (a t)").unsqueeze(2).to_broadcast([P, 2 * PACK, GROUPS])
         nc.vector.tensor_tensor(out=all_rows[:, :, 0:GROUPS, 0], in0=raised_wide, in1=factors_flat, op=ALU.mult)
@@ -402,7 +408,9 @@ def tile_gaussianlayer_t_kernel(tc, x, mus, log_vars, weights, out):
         turned = psum.tile([P, 2 * PACK, P], BF16, name="turned", tag="bank")
         for q in range(2 * PACK):
             nc.tensor.transpose(turned[:, q, :], coef_t[:, q, :], ident_bf[:])
-        nc.scalar.copy(out=coef_rows[:, 0:PACK, :], in_=turned[:, 0:PACK, :])
+        nc.scalar.copy(out=coef_rows[:, 0:1, :], in_=turned[:, 0:1, :])
+        nc.scalar.copy(out=coef_rows[:, 1:PACK, :], in_=turned[:, 1:PACK, :])
+        nc.vector.reduce_sum(out=w_sum[:], in_=w_ps[:, 0:PACK], axis=mybir.AxisListType.X)
         quantise_x(0)
         nc.vector.tensor_copy(out=coef_rows[:, PACK : 2 * PACK, :], in_=turned[:, PACK : 2 * PACK, :])
         for t in range(PACK // 2):
@@ -476,6 +484,8 @@ def tile_gaussianlayer_t_kernel(tc, x, mus, log_vars, weights, out):
                     weigh(i, r)
                 elif kind == "S":
                     weigh_away(i, r)
+                elif kind == "A":
+                    weigh_scalar(i, r)
                 elif kind == "C":
                     quantise_c(i - 1, 0, ROWS)
                 elif kind == "c":

import math
from contextlib import ExitStack

import concourse.mybir as mybir
from concourse.masks import make_identity

F32 = mybir.dt.float32
BF16 = mybir.dt.bfloat16
U32 = mybir.dt.uint32
U8 = mybir.dt.uint8
FP8X4 = mybir.dt.float8_e4m3fn_x4
ACT = mybir.ActivationFunctionType
ALU = mybir.AluOpType

BATCH, IN, OUT, COMPS = 8192, 1024, 256, 512
FLOPS = 2 * BATCH * IN * COMPS + 2 * BATCH * COMPS * OUT

P = 128
PACK = 4
K_PASS = P * PACK
TURNED = (8, 14)
BLOCK = 32
PRE = {5: [(8, 0, 8)], 6: [(8, 8, 8)]}
STEPLOAD = {5: [(14, 0, 4)], 6: [(14, 4, 4)], 7: [(14, 8, 4)], 8: [(14, 12, 4)]}
UP = 3
TURN_TOKEN = "w3"
BANKS = 8
HALF_IN = IN // 2
PASSES = IN // K_PASS
ROWS = 4
HALVES = 2
HALF_ROWS = ROWS // HALVES
CHUNK = ROWS * P
N_CHUNKS = BATCH // CHUNK
X_BUFS = 8
PRELOAD = 7
IN_BLOCKS = IN // (2 * P)
OUT_BLOCKS = OUT // P
N_BLOCKS = 2 * IN_BLOCKS + OUT_BLOCKS
STEPS = (2 * P, P)
PIECES = 3
STRIDE = 4
GROUPS = 2 + 2 * IN_BLOCKS
LINEAR_ROW = 2 * STRIDE
CONST_ROW = LINEAR_ROW + IN_BLOCKS * STRIDE
NORM_ROW = 64
AWAY = 1
FIRST = "M0 w0 C M1 x S1 M2 w2 M3 w3 G0 G1 T0 T1 T2 T3 g"
EARLY = "C M0 w0 M1 O x S1 M2 w2 M3 w3 O T0 T1 T2 T3"
STEADY = "C M0 w0 M1 O x S1 M2 w2 M3 w3 O T0 T1 T2 T3"
ENDQ = (3,)
NEXT = "C M0 w0 M1 O x S1 M2 w2 M3 w3 O T0 T1 T2 T3"
LAST = "C M0 w0 O M1 w1 O c0 M2 w2 O c1 M3 w3 O c2"
LOOKAHEAD = 2


def tile_gaussianlayer_t_kernel(tc, x, mus, log_vars, weights, out):
    nc = tc.nc
    with ExitStack() as ctx:
        keep = ctx.enter_context(tc.tile_pool(name="keep", bufs=1))
        x_pool = ctx.enter_context(tc.tile_pool(name="x_pool", bufs=X_BUFS))
        stream = ctx.enter_context(tc.tile_pool(name="stream", bufs=3))
        turned_pool = ctx.enter_context(tc.tile_pool(name="turned_pool", bufs=1))
        tx_pool = ctx.enter_context(tc.tile_pool(name="tx_pool", bufs=2))
        psum = ctx.enter_context(tc.psum_pool(name="psum", bufs=BANKS))
        ctx.enter_context(tc.manual_schedule())

        mus_sb = keep.tile([P, PACK * 2], BF16, name="mus_sb")
        nc.sync.dma_start(out=mus_sb[:], in_=mus.rearrange("(p t) c -> p (t c)", t=PACK))
        lv_sb = keep.tile([P, PACK * 2], BF16, name="lv_sb")
        nc.sync.dma_start(out=lv_sb[:], in_=log_vars.rearrange("(p t) c -> p (t c)", t=PACK))

        w_sb = keep.tile([P, PACK], BF16, name="w_sb")
        nc.sync.dma_start(out=w_sb[:], in_=weights.rearrange("(p t) -> p t", t=PACK))

        x_tiles = {}

        turned_x = {}

        def load_turned(c, first_piece, count):
            if first_piece == 0:
                turned_x[c] = tx_pool.tile([P, ROWS * IN], BF16, name="turned_x", align_bytes=64)
            rows = x[c * CHUNK : (c + 1) * CHUNK, :].rearrange("(j b) k -> b j k", b=BLOCK // 2)
            for piece in range(first_piece, first_piece + count):
                g, u, q = piece // 8, piece // 4 % 2, piece % 4
                first = g * K_PASS + u * 2 * P + q * 2 * BLOCK
                width = ROWS * IN // PASSES
                nc.sync.dma_start(
                    out=turned_x[c][q * BLOCK + u : (q + 1) * BLOCK : 2, g * width : (g + 1) * width].rearrange(
                        "p (j w) -> p j w", w=2 * BLOCK
                    ),
                    in_=rows[:, :, first : first + 2 * BLOCK],
                )

        def load_chunk(c, pieces=1):
            if c in TURNED:
                return
            x_sb = x_pool.tile([P, ROWS * IN], BF16, name="x_sb")
            rows = x[c * CHUNK : (c + 1) * CHUNK, :].rearrange("(p r) k -> p (r k)", r=ROWS)
            width = ROWS * IN // pieces
            for piece in range(pieces):
                cols = slice(piece * width, (piece + 1) * width)
                nc.sync.dma_start(out=x_sb[:, cols], in_=rows[:, cols])
            x_tiles[c] = x_sb

        load_chunk(0, pieces=2)
        for c in range(1, PRELOAD):
            load_chunk(c)
            for a, b, n in PRE.get(c, ()):
                load_turned(a, b, n)

        twos = keep.tile([P, 2 * PACK], F32, name="twos")
        nc.vector.memset(twos[:], 2.0)
        warm_out = keep.tile([P, 1], F32, name="warm_out")
        nc.scalar.activation(out=warm_out[:], in_=twos[:, 0:1], func=ACT.Exp)
        offset = keep.tile([P, N_BLOCKS], F32, name="offset")
        in_blocks = offset[:, 0 : 2 * IN_BLOCKS].rearrange("p (e b) -> p e b", e=2)
        nc.gpsimd.iota(
            in_blocks, pattern=[[1, 2], [0, IN_BLOCKS]], base=-P, channel_multiplier=2,
            allow_small_or_imprecise_dtypes=True,
        )
        nc.gpsimd.iota(
            offset[:, 2 * IN_BLOCKS : N_BLOCKS], pattern=[[0, OUT_BLOCKS]], base=-P // 2, channel_multiplier=1,
            allow_small_or_imprecise_dtypes=True,
        )
        ident_bf = keep.tile([P, P], BF16, name="ident_bf")
        make_identity(nc, ident_bf[:])
        ident_f32 = keep.tile([P, P], F32, name="ident_f32")
        make_identity(nc, ident_f32[:])
        middle = keep.tile([P, 2, IN_BLOCKS], F32, name="middle")
        for axis in range(2):
            nc.gpsimd.iota(
                middle[:, axis, :], pattern=[[STEPS[axis], IN_BLOCKS]], base=STEPS[axis] // 2, channel_multiplier=0,
                allow_small_or_imprecise_dtypes=True,
            )
        basis_t = keep.tile([P, N_BLOCKS * P + P], BF16, name="basis_t")
        nc.vector.memset(basis_t[:].bitcast(F32), 0.0)
        coef_t = keep.tile([P, 2 * PACK, P], BF16, name="coef_t")
        square = keep.tile([P, N_BLOCKS], F32, name="square")
        nc.vector.tensor_tensor(out=square[:], in0=offset[:], in1=offset[:], op=ALU.mult)
        by_block = basis_t[:, 0 : N_BLOCKS * P].rearrange("p (n k) -> p n k", k=P)
        wide = [P, N_BLOCKS, PIECES]
        nc.scalar.copy(out=by_block[:, :, 0:PIECES], in_=square[:].unsqueeze(2).to_broadcast(wide))
        nc.vector.memset(coef_t[:].rearrange("p q k -> p (q k)").bitcast(F32), 0.0)

        def staircase(first, count, row):
            step = P + STRIDE
            run = basis_t[:, first * P : first * P + count * step].rearrange("p (b k) -> p b k", k=step)
            return run[:, :, row : row + PIECES]

        groups = ((0, IN_BLOCKS), (IN_BLOCKS, IN_BLOCKS), (2 * IN_BLOCKS, OUT_BLOCKS))
        for first, count in groups:
            nc.scalar.copy(
                out=staircase(first, count, LINEAR_ROW),
                in_=offset[:, first : first + count].unsqueeze(2).to_broadcast([P, count, PIECES]),
            )
        for first, count in groups:
            nc.vector.memset(staircase(first, count, CONST_ROW), 1.0)
        nc.vector.memset(by_block[:, :, NORM_ROW : NORM_ROW + PIECES], 1.0)
        nc.vector.tensor_tensor(
            out=by_block[:, :, STRIDE : STRIDE + PIECES], in0=square[:].unsqueeze(2).to_broadcast(wide),
            in1=by_block[:, :, 0:PIECES], op=ALU.subtract,
        )
        spread_bf = keep.tile([P, P], BF16, name="spread_bf")
        nc.vector.memset(spread_bf[:], float(IN))
        factors = keep.tile([P, 2, PACK, GROUPS], F32, name="factors")
        spans = (IN - 1, OUT - 1)
        steep = [-0.5 / float(span * span) for span in spans]
        for axis in range(2):
            nc.vector.tensor_scalar(
                out=factors[:, axis, :, 0:2], in0=twos[:].rearrange("p (t a) -> p t a", a=2),
                scalar1=0.5 * steep[axis], scalar2=None, op0=ALU.mult,
            )

        lv_by_axis = lv_sb[:].rearrange("p (t a) -> p a t", a=2)
        mus_by_axis = mus_sb[:].rearrange("p (t a) -> p a t", a=2)
        power = keep.tile([P, 2, PACK], F32, name="power")
        nc.gpsimd.tensor_scalar(
            out=power[:], in0=lv_by_axis, scalar1=-1.0 / math.log(2.0), scalar2=0.0, op0=ALU.mult, op1=ALU.add
        )
        raised = keep.tile([P, 2, PACK], F32, name="raised")
        nc.gpsimd.tensor_tensor(
            out=raised[:], in0=twos[:].rearrange("p (a t) -> p a t", a=2), in1=power[:], op=ALU.pow
        )
        distance = keep.tile([P, 2, PACK, IN_BLOCKS], F32, name="distance")
        for axis in range(2):
            nc.vector.scalar_tensor_tensor(
                out=distance[:, axis], in0=mus_by_axis[:, axis, :].unsqueeze(2).to_broadcast([P, PACK, IN_BLOCKS]),
                scalar=-float(spans[axis]), in1=middle[:, axis, :].unsqueeze(1).to_broadcast([P, PACK, IN_BLOCKS]),
                op0=ALU.mult, op1=ALU.add,
            )
        norm = keep.tile([P, 2 * PACK, 1], F32, name="norm")
        nc.vector.tensor_scalar(
            out=norm[:].rearrange("p (a t) o -> p a (t o)", a=2), in0=lv_by_axis, scalar1=-0.5,
            scalar2=-0.5 * math.log(2.0 * math.pi), op0=ALU.mult, op1=ALU.add,
        )
        all_rows = coef_t[:].rearrange("p q (g j) -> p q g j", j=STRIDE)
        factors_flat = factors[:].rearrange("p a t g -> p (a t) g")
        blocks = [P, 2 * PACK, IN_BLOCKS]
        flat_distance = distance[:].rearrange("p a t b -> p (a t) b")
        nc.vector.scalar_tensor_tensor(
            out=factors_flat[:, :, 2 : 2 + IN_BLOCKS], in0=flat_distance, scalar=2.0,
            in1=factors_flat[:, :, 0:1].to_broadcast(blocks), op0=ALU.mult, op1=ALU.mult,
        )
        nc.vector.tensor_copy(out=all_rows[:, :, NORM_ROW // STRIDE, 0:1], in_=norm[:])
        nc.vector.scalar_tensor_tensor(
            out=factors_flat[:, :, 2 + IN_BLOCKS : GROUPS], in0=factors_flat[:, :, 2 : 2 + IN_BLOCKS],
            scalar=0.5, in1=flat_distance, op0=ALU.mult, op1=ALU.mult,
        )

        def split(value, first, count):
            rows = all_rows[:, :, first : first + count, :]
            rest = keep.tile([P, 2 * PACK, count], F32, name="rest%d" % first)
            nc.vector.tensor_tensor(out=rest[:], in0=value, in1=rows[:, :, :, 0], op=ALU.subtract)
            nc.vector.tensor_tensor(out=rows[:, :, :, 1], in0=value, in1=rows[:, :, :, 0], op=ALU.subtract)
            nc.vector.tensor_tensor(out=rows[:, :, :, 2], in0=rest[:], in1=rows[:, :, :, 1], op=ALU.subtract)

        w_f32 = keep.tile([P, PACK], F32, name="w_f32")
        nc.gpsimd.tensor_copy(out=w_f32[:], in_=w_sb[:])

        xt_banks, gx_tiles, xc_tiles, xs_tiles = {}, {}, {}, {}
        gc_tiles, cc_tiles, cs_tiles = {}, {}, {}
        c_banks, o_banks = {}, {}

        def transpose_rows(c, r):
            words = x_tiles[c][:].bitcast(F32)
            xt = psum.tile([P, PACK, P], F32, name="xt", tag="bank")
            for q in range(PACK):
                first = r * HALF_IN + q * P
                nc.tensor.transpose(xt[:, q, :], words[:, first : first + P], ident_f32[:])
            xt_banks[(c, r)] = xt

        def copy_rows(c, r, copy_out):
            if r == 0:
                gx_tiles[c] = stream.tile([P, ROWS * IN], BF16, name="gx", align_bytes=64)
            gx_words = gx_tiles[c][:].bitcast(F32)
            copy_out(
                out=gx_words[:, r * HALF_IN : (r + 1) * HALF_IN].rearrange("p (g b u) -> p g b u", g=PASSES, u=2),
                in_=xt_banks[(c, r)][:].rearrange("p (g u) b -> p g b u", u=2),
            )

        def turn_rows(c, r):
            if r == 0:
                gx_tiles[c] = turned_pool.tile([P, ROWS * IN], BF16, name="gx_turned", align_bytes=64)
            words = slice(r * HALF_IN, (r + 1) * HALF_IN)
            nc.vector.transpose(out=gx_tiles[c][:].bitcast(F32)[:, words], in_=turned_x[c][:].bitcast(F32)[:, words])

        def quantise_x(c):
            xc = stream.tile([P, ROWS * PASSES * P], U32, name="xc", align_bytes=256, bufs=LOOKAHEAD + 2)
            xs = stream.tile([P, ROWS * PASSES * P], U8, name="xs", align_bytes=256, bufs=LOOKAHEAD + 2)
            nc.vector.quantize_mx(out=xc[:].bitcast(FP8X4), scales=xs[:], in_=gx_tiles[c][:])
            xc_tiles[c], xs_tiles[c] = xc, xs

        def first_matmul(c, r, t):
            for g in range(PASSES):
                w_cols = slice((t * PASSES + g) * P, (t * PASSES + g + 1) * P)
                first = g * ROWS + r if c in TURNED else r * PASSES + g
                x_cols = slice(first * P, (first + 1) * P)
                nc.tensor.matmul_mx(
                    out=c_banks[(c, r)][:, t, :],
                    lhsT=gin_c[:, w_cols].bitcast(FP8X4),
                    lhsT_scale=gin_s[:, w_cols],
                    rhs=xc_tiles[c][:, x_cols].bitcast(FP8X4),
                    rhs_scale=xs_tiles[c][:, x_cols],
                    start=(g == 0),
                    stop=(g == PASSES - 1),
                )

        def open_c(c):
            gc_tiles[c] = stream.tile([P, ROWS * COMPS], BF16, name="gc", align_bytes=64)
            cc_tiles[c] = stream.tile([P, ROWS * P], U32, name="cc", align_bytes=256)
            cs_tiles[c] = stream.tile([P, ROWS * P], U8, name="cs", align_bytes=256)

        def weigh(c, r):
            nc.vector.tensor_tensor(
                out=gc_tiles[c][:, r * COMPS : (r + 1) * COMPS].rearrange("p (b t) -> p b t", t=PACK),
                in0=c_banks[(c, r)][:].rearrange("p t b -> p b t"),
                in1=w_f32[:].unsqueeze(1).to_broadcast([P, P, PACK]),
                op=ALU.mult,
            )

        def weigh_away(c, r):
            plain = stream.tile([P, COMPS], F32, name="plain")
            nc.scalar.copy(
                out=plain[:].rearrange("p (b t) -> p b t", t=PACK), in_=c_banks[(c, r)][:].rearrange("p t b -> p b t")
            )
            nc.gpsimd.tensor_tensor(
                out=gc_tiles[c][:, r * COMPS : (r + 1) * COMPS].rearrange("p (b t) -> p b t", t=PACK),
                in0=plain[:].rearrange("p (b t) -> p b t", t=PACK),
                in1=w_f32[:].unsqueeze(1).to_broadcast([P, P, PACK]),
                op=ALU.mult,
            )

        def weigh_scalar(c, r):
            values = gc_tiles[c][:, r * COMPS : (r + 1) * COMPS].rearrange("p (b t) -> p b t", t=PACK)
            for t in range(PACK):
                nc.scalar.activation(
                    out=values[:, :, t], in_=c_banks[(c, r)][:, t, :], func=ACT.Copy, scale=w_f32[:, t : t + 1]
                )

        def quantise_c(c, first, rows=HALF_ROWS):
            words = slice(first * P, (first + rows) * P)
            values = slice(first * COMPS, (first + rows) * COMPS)
            nc.vector.quantize_mx(
                out=cc_tiles[c][:, words].bitcast(FP8X4), scales=cs_tiles[c][:, words], in_=gc_tiles[c][:, values]
            )

        def second_matmul(c, first, rows=HALF_ROWS):
            o_ps = psum.tile([P, HALF_ROWS * OUT], F32, name="o_ps", tag="bank")
            for s in range(rows):
                r = first + s
                nc.tensor.matmul_mx(
                    out=o_ps[:, s * OUT : (s + 1) * OUT],
                    lhsT=cc_tiles[c][:, r * P : (r + 1) * P].bitcast(FP8X4),
                    lhsT_scale=cs_tiles[c][:, r * P : (r + 1) * P],
                    rhs=gout_c[:].bitcast(FP8X4),
                    rhs_scale=gout_s[:],
                    start=True,
                    stop=True,
                )
            o_banks[(c, first)] = o_ps

        def store_rows(c, first, rows=HALF_ROWS, on_vector=False):
            o_sb = stream.tile([P, HALF_ROWS * OUT], F32, name="o_sb", bufs=8)
            cols = slice(0, rows * OUT)
            bank = o_banks[(c, first)][:, cols]
            if on_vector:
                nc.vector.tensor_scalar(
                    out=o_sb[:, cols], in0=bank, scalar1=inv_divisor[:, 0:1], scalar2=None, op0=ALU.mult
                )
            else:
                nc.scalar.activation(out=o_sb[:, cols], in_=bank, func=ACT.Copy, scale=inv_divisor[:, 0:1])
            chunk = out[c * CHUNK : (c + 1) * CHUNK, :]
            if c in TURNED:
                chunk = chunk.rearrange("(r p) j -> p r j", p=P)
            else:
                chunk = chunk.rearrange("(p r) j -> p r j", r=ROWS)
            nc.sync.dma_start(
                out=chunk[:, first : first + rows, :], in_=o_sb[:, cols].rearrange("p (r j) -> p r j", j=OUT)
            )

        gg_in = keep.tile([P, PACK * PASSES * P * PACK], BF16, name="gg_in", align_bytes=64)
        gin_c = keep.tile([P, PACK * PASSES * P], U32, name="gin_c", align_bytes=256)
        gin_s = keep.tile([P, PACK * PASSES * P], U8, name="gin_s", align_bytes=256)
        basis = keep.tile([P, N_BLOCKS, P], BF16, name="basis")
        coef_rows = keep.tile([P, 2 * PACK, P], BF16, name="coef_rows")
        e_banks = {}

        def turn(out_tile, source, first, count, copy_out):
            turned = psum.tile([P, PASSES * PACK, P], BF16, name="turned", tag="bank")
            for n in range(count):
                nc.tensor.transpose(turned[:, n, :], source[:, first + n, :], ident_bf[:])
            copy_out(out=out_tile[:, first : first + count, :], in_=turned[:, 0:count, :])

        def exponents_in(t, g):
            e_ps = psum.tile([P, PACK, P], F32, name="e_ps", tag="bank")
            for u in range(2):
                for e in range(2):
                    nc.tensor.matmul(
                        out=e_ps[:, 2 * u + e, :], lhsT=basis[:, e * IN_BLOCKS + 2 * g + u, :], rhs=coef_rows[:, t, :],
                        start=True, stop=True,
                    )
            e_banks[(t, g)] = e_ps

        def gauss_in(t, g):
            words = slice((t * PASSES + g) * COMPS, (t * PASSES + g + 1) * COMPS)
            nc.scalar.activation(
                out=gg_in[:, words].rearrange("p (m k) -> p m k", k=PACK),
                in_=e_banks[(t, g)][:].rearrange("p k m -> p m k"), func=ACT.Exp,
            )

        def quantise_gauss(t):
            words = slice(t * PASSES * P, (t + 1) * PASSES * P)
            nc.vector.quantize_mx(
                out=gin_c[:, words].bitcast(FP8X4), scales=gin_s[:, words], in_=gg_in[:, t * IN : (t + 1) * IN]
            )

        def gauss_out(h):
            e_ps = psum.tile([P, PACK, P], F32, name="e_ps", tag="bank")
            for t in range(PACK):
                nc.tensor.matmul(
                    out=e_ps[:, t, :], lhsT=coef_rows[:, PACK + t, :], rhs=basis[:, 2 * IN_BLOCKS + h, :],
                    start=True, stop=True,
                )
            nc.scalar.activation(
                out=gg_out[:, h * P : (h + 1) * P, :], in_=e_ps[:].rearrange("p t j -> p j t"), func=ACT.Exp
            )

        gg_out = keep.tile([P, OUT, PACK], BF16, name="gg_out", align_bytes=64)
        gout_c = keep.tile([P, OUT], U32, name="gout_c", align_bytes=256)
        gout_s = keep.tile([P, OUT], U8, name="gout_s", align_bytes=256)

        turn(basis, by_block, 0, 2 * IN_BLOCKS, nc.scalar.copy)
        turn(basis, by_block, 2 * IN_BLOCKS, OUT_BLOCKS, nc.scalar.copy)
        w_ps = psum.tile([P, HALF_ROWS * OUT], F32, name="w_ps", tag="bank")
        nc.tensor.matmul(out=w_ps[:, 0:PACK], lhsT=spread_bf[:], rhs=w_sb[:], start=True, stop=True)
        w_sum = keep.tile([P, 1], F32, name="w_sum")
        inv_divisor = keep.tile([P, 1], F32, name="inv_divisor")
        split(norm[:], NORM_ROW // STRIDE, 1)
        coef = keep.tile([P, 2 * PACK, GROUPS], F32, name="coef")
        raised_wide = raised[:].rearrange("p a t -> p (a t)").unsqueeze(2).to_broadcast([P, 2 * PACK, GROUPS])
        nc.vector.tensor_tensor(out=all_rows[:, :, 0:GROUPS, 0], in0=raised_wide, in1=factors_flat, op=ALU.mult)
        nc.vector.tensor_tensor(out=coef[:], in0=raised_wide, in1=factors_flat, op=ALU.mult)
        split(coef[:], 0, GROUPS)
        for r in range(ROWS):
            transpose_rows(0, r)
            copy_rows(0, r, nc.scalar.copy if r < 2 else nc.vector.tensor_copy)
        turned = psum.tile([P, 2 * PACK, P], BF16, name="turned", tag="bank")
        for q in range(2 * PACK):
            nc.tensor.transpose(turned[:, q, :], coef_t[:, q, :], ident_bf[:])
        nc.scalar.copy(out=coef_rows[:, 0:1, :], in_=turned[:, 0:1, :])
        nc.scalar.copy(out=coef_rows[:, 1:PACK, :], in_=turned[:, 1:PACK, :])
        nc.vector.reduce_sum(out=w_sum[:], in_=w_ps[:, 0:PACK], axis=mybir.AxisListType.X)
        quantise_x(0)
        nc.vector.tensor_copy(out=coef_rows[:, PACK : 2 * PACK, :], in_=turned[:, PACK : 2 * PACK, :])
        for t in range(PACK // 2):
            for g in range(PASSES):
                exponents_in(t, g)
                gauss_in(t, g)
        for r in range(ROWS):
            transpose_rows(1, r)
        copy_rows(1, 0, nc.vector.tensor_copy)
        quantise_gauss(0)
        copy_rows(1, 1, nc.vector.tensor_copy)
        quantise_gauss(1)
        for r in range(HALF_ROWS, ROWS):
            copy_rows(1, r, nc.vector.tensor_copy)
        for t in range(PACK // 2, PACK):
            for g in range(PASSES):
                exponents_in(t, g)
                gauss_in(t, g)
        quantise_gauss(2)
        quantise_gauss(3)
        quantise_x(1)
        for r in range(ROWS):
            c_ps = psum.tile([P, PACK, P], F32, name="c_ps", tag="bank")
            c_banks[(0, r)] = c_ps
        for t in range(PACK // 2):
            for r in range(HALF_ROWS):
                first_matmul(0, r, t)
        for r in range(HALF_ROWS):
            transpose_rows(2, r)
        for t in range(PACK // 2):
            for r in range(HALF_ROWS, ROWS):
                first_matmul(0, r, t)
        for r in range(ROWS):
            first_matmul(0, r, 2)
        for r in range(ROWS):
            first_matmul(0, r, 3)
        for r in range(HALF_ROWS, ROWS):
            transpose_rows(2, r)
        for r in range(HALF_ROWS):
            copy_rows(2, r, nc.scalar.copy)
        open_c(0)
        weigh(0, 0)
        nc.vector.reciprocal(out=inv_divisor[:], in_=w_sum[:])
        weigh_away(0, 1)
        weigh(0, 2)
        weigh(0, 3)
        for r in range(HALF_ROWS, ROWS):
            copy_rows(2, r, nc.scalar.copy)

        halves_done = 0
        upright = [(c, r) for c in range(LOOKAHEAD + 1, N_CHUNKS) if c not in TURNED for r in range(ROWS)]
        rows_done = 0
        turn_list = [(c, r) for c in TURNED for r in range(ROWS)]
        turns_done = 0
        for i in range(1, N_CHUNKS):
            last = i == N_CHUNKS - 1
            open_c(i)
            if i - 1 + PRELOAD < N_CHUNKS:
                load_chunk(i - 1 + PRELOAD)
            for a, b, n in STEPLOAD.get(i, ()):
                load_turned(a, b, n)
            steps = FIRST if i == 1 else EARLY if i <= 3 else LAST if last else NEXT if i == N_CHUNKS - 2 else STEADY
            for token in steps.split():
                kind, r = token[0], int(token[1:] or 0)
                if kind == "M":
                    c_ps = psum.tile([P, PACK, P], F32, name="c_ps", tag="bank")
                    c_banks[(i, r)] = c_ps
                    for t in range(PACK):
                        first_matmul(i, r, t)
                elif kind == "w":
                    weigh(i, r)
                elif kind == "S":
                    weigh_away(i, r)
                elif kind == "A":
                    weigh_scalar(i, r)
                elif kind == "C":
                    quantise_c(i - 1, 0, ROWS)
                elif kind == "c":
                    quantise_c(i, r, 1)
                elif kind == "h":
                    quantise_c(0, HALF_ROWS)
                elif kind == "x":
                    quantise_x(i + 1)
                elif kind == "g":
                    nc.vector.quantize_mx(
                        out=gout_c[:].bitcast(FP8X4), scales=gout_s[:], in_=gg_out[:].rearrange("p j t -> p (j t)")
                    )
                elif kind == "G":
                    gauss_out(r)
                elif kind == "O":
                    chunk, half = divmod(halves_done, HALVES)
                    second_matmul(chunk, half * HALF_ROWS)
                    store_rows(chunk, half * HALF_ROWS)
                    halves_done += 1
                elif kind == "T" and r == 0:
                    needed = len([c for c, rr in upright if c <= i + LOOKAHEAD])
                    due = max(needed, min(rows_done + UP, len(upright)))
                    while rows_done < due:
                        c, rr = upright[rows_done]
                        transpose_rows(c, rr)
                        copy_rows(c, rr, nc.scalar.copy)
                        rows_done += 1
                for a in TURNED:
                    if token == TURN_TOKEN and 0 <= i - a + 5 < ROWS:
                        turn_rows(a, i - a + 5)
        while halves_done < HALVES * (N_CHUNKS - 1):
            chunk, half = divmod(halves_done, HALVES)
            second_matmul(chunk, half * HALF_ROWS)
            store_rows(chunk, half * HALF_ROWS)
            halves_done += 1
        for r in ENDQ:
            quantise_c(N_CHUNKS - 1, r, 1)
        for r in range(ROWS):
            second_matmul(N_CHUNKS - 1, r, 1)
            store_rows(N_CHUNKS - 1, r, 1, on_vector=(r == ROWS - 1))
